import numpy as np
import ml_dtypes


def mxq(x, axis, fmt="e4m3"):
    dtype, down = {"e4m3": (ml_dtypes.float8_e4m3fn, 7), "e5m2": (ml_dtypes.float8_e5m2, 14)}[fmt]
    v = np.moveaxis(np.asarray(x, np.float32).astype(ml_dtypes.bfloat16).astype(np.float64), axis, -1)
    blocks = v.reshape(v.shape[:-1] + (-1, 32))
    amax = np.abs(blocks).max(-1, keepdims=True)
    byte = np.maximum(np.where(amax > 0, np.frexp(amax)[1] - 1 + 127, 0) - down, 1)
    scale = np.exp2(byte - 127.0)
    codes = (blocks / scale).astype(np.float32).astype(dtype).astype(np.float64)
    return np.moveaxis((codes * scale).reshape(v.shape), -1, axis)


WIDE = False


def mx_kscale(k):
    if not WIDE:
        return np.ones(k)
    levels = np.array([10, -10, 5, -5, 0])
    if k % 512:
        return np.exp2(np.random.permutation(np.resize(levels, k // 32))).repeat(32)
    a = np.empty((k // 512, 16))
    for p in range(k // 512):
        a[p, :8] = np.random.permutation(np.resize(levels, 8))
        for g in range(8):
            far = levels[np.abs(levels - a[p, g]) >= 10]
            a[p, g + 8] = far[np.random.randint(len(far))]
    return np.exp2(a.ravel()).repeat(32)


BF16 = ml_dtypes.bfloat16


def bf(x):
    return np.asarray(x, np.float32).astype(BF16)


def f64(x):
    return np.asarray(x).astype(np.float64)


B, H, L, E, QD = 16, 1, 128, 2048, 128
EPS = 1e-5


def build_decay_mask(num_heads, max_len):
    r = f64(np.arange(max_len))
    dec = np.array([1.0 - 2.0 ** (-5 - h) for h in range(num_heads)])
    expo = r[None, :] - r[:, None]
    return np.where(r[:, None] >= r[None, :], dec[:, None, None] ** expo[None], 0.0)


def setup_inputs():
    s = mx_kscale(E)
    kv = (0.1 + 0.32 * np.random.standard_normal((B, H, L, QD))) * (0.1 + 0.32 * np.random.standard_normal((B, H, L, QD)))
    return {"x": bf(np.random.standard_normal((B, H, L, E)) * s),
            "Wq": bf(np.random.standard_normal((QD, E)) / np.sqrt(E) / s),
            "bq": bf(0.3 + 0.3 * np.random.standard_normal(QD)),
            "kv": bf(kv),
            "decay_mask": bf(build_decay_mask(H, L))}


def core(x, Wq, bq, kv, decay_mask):
    b, h, l, e = x.shape
    Q = (mxq(f64(x), 3, "e4m3") @ mxq(f64(Wq), 1, "e4m3").T) + f64(bq)
    D = f64(decay_mask)[0, :l, :l]
    y = Q * (f64(kv) @ D.T)
    mean = y.mean(axis=(2, 3), keepdims=True)
    var = ((y - mean) ** 2).mean(axis=(2, 3), keepdims=True)
    y = (y - mean) / np.sqrt(var + EPS)
    return y.reshape(b, l, -1)


def e4m3fn_bytes(y):
    return np.clip(np.asarray(y, np.float64), -448.0, 448.0).astype(np.float32).astype(ml_dtypes.float8_e4m3fn).view(np.uint8)


def reference(x, Wq, bq, kv, decay_mask):
    out = core(x, Wq, bq, kv, decay_mask)
    s = np.max(np.abs(out), axis=-1, keepdims=True) / 448.0
    return out, e4m3fn_bytes(out / s)

@@ -1,0 +1,373 @@
+from contextlib import ExitStack
+
+import concourse.mybir as mybir
+from concourse.masks import make_block_diagonal, make_identity
+
+F32 = mybir.dt.float32
+BF16 = mybir.dt.bfloat16
+U32 = mybir.dt.uint32
+U8 = mybir.dt.uint8
+FP8 = mybir.dt.float8_e4m3fn
+FP8X4 = mybir.dt.float8_e4m3fn_x4
+ALU = mybir.AluOpType
+ACT = mybir.ActivationFunctionType
+AXIS = mybir.AxisListType
+
+B, L, E, QD = 16, 128, 2048, 128
+EPS = 1e-5
+P = 128
+PASSES = E // (4 * P)
+FLOPS = 2 * B * L * E * QD + 2 * B * L * L * QD
+
+GROUPS = (4, 4, 4, 4)
+RUN = 2
+SCALAR_CASTS = (1, 3)
+
+
+def tile_parallelretention_pb_kernel(tc, x, Wq, bq, kv, decay_mask, out_0, out_1):
+    nc = tc.nc
+    x_rows = x.rearrange("b h l e -> (b h l) e")
+    kv_rows = kv.rearrange("b h l k -> (b h l) k")
+    o0_rows = out_0.rearrange("b l q -> (b l) q")
+    o1_rows = out_1.rearrange("b l q -> (b l) q")
+
+    groups = []
+    tiles = []
+    for n in GROUPS:
+        groups.append((P * len(tiles), n, len(tiles)))
+        for j in range(n):
+            tiles.append((len(groups) - 1, j))
+    n_tiles = len(tiles)
+    assert n_tiles == B
+
+    with ExitStack() as ctx:
+        const = ctx.enter_context(tc.tile_pool(name="const", bufs=1))
+        xin = ctx.enter_context(tc.tile_pool(name="xin", bufs=1))
+        work = ctx.enter_context(tc.tile_pool(name="work", bufs=2))
+        tp = ctx.enter_context(tc.psum_pool(name="tp", bufs=5))
+        gp = ctx.enter_context(tc.psum_pool(name="gp", bufs=1))
+        qp = ctx.enter_context(tc.psum_pool(name="qp", bufs=2))
+
+        ident_b = const.tile([P, P], BF16, name="ident_b")
+        ident_f = const.tile([P, P], F32, name="ident_f")
+        ones_b = const.tile([P, P], BF16, name="ones_b")
+        brow = const.tile([P, QD], BF16, name="brow")
+        zero_col = const.tile([P, 1], F32, name="zero_col")
+        eps_col = const.tile([P, 1], F32, name="eps_col")
+        warm = const.tile([P, 1], F32, name="warm")
+        nc.vector.memset(brow[:], 0.0)
+        nc.vector.memset(eps_col[:], EPS)
+        nc.vector.memset(ones_b[:], 1.0)
+        nc.vector.memset(zero_col[:], 0.0)
+        nc.scalar.activation(out=warm[:], in_=eps_col[:], func=ACT.Sqrt)
+        make_identity(nc, ident_b[:])
+        make_identity(nc, ident_f[:])
+        sum_mask = {}
+        for n in GROUPS:
+            if n not in sum_mask:
+                blockdiag = const.tile([P, P], F32, name="blockdiag%d" % n)
+                if n == 1:
+                    nc.vector.memset(blockdiag[:], 1.0)
+                else:
+                    make_block_diagonal(nc, blockdiag[:], P // n)
+                sum_mask[n] = blockdiag
+
+        d_in = xin.tile([P, L], BF16, name="d_in")
+        kv_in = [xin.tile([P, n, L], BF16, name="kv_in%d" % g) for g, (r0, n, i0) in enumerate(groups)]
+        w_in = [xin.tile([P, E // 2], BF16, name="w_in%d" % h) for h in range(2)]
+        x_in = [[xin.tile([P, E // 2], BF16, name="x_in%d_%d" % (i, h)) for h in range(2)] for i in range(n_tiles)]
+        kvT = [const.tile([P, n, P], BF16, name="kvT%d" % g) for g, (r0, n, i0) in enumerate(groups)]
+        dT = const.tile([P, QD], BF16, name="dT")
+        b4 = const.tile([P, 4, QD], F32, name="b4")
+        w_grouped = const.tile([P, E], BF16, name="w_grouped", align_bytes=64)
+        w_codes = const.tile([P, E // 4], U32, name="w_codes", align_bytes=64)
+        w_scales = const.tile([P, E // 4], U8, name="w_scales", align_bytes=64)
+
+        banks = {}
+        grouped = {}
+        codes = {}
+        scales = {}
+        q_ps = {}
+        ep = {}
+
+        def transpose_half(key, words):
+            bank = tp.tile([P, 2, 2, P], F32, tag="tp", name="xT")
+            for c in range(2):
+                for u in range(2):
+                    nc.tensor.transpose(bank[:, c, u, :], words[:, 256 * c + u : 256 * (c + 1) : 2], ident_f[:])
+            banks[key] = bank
+
+        def copy_half(key, dst_tile, h, on_scalar):
+            dst = dst_tile[:].bitcast(F32)[:, 512 * h : 512 * (h + 1)].rearrange("p (c r u) -> p c r u", c=2, u=2)
+            src = banks[key][:].rearrange("p c u r -> p c r u")
+            if on_scalar:
+                nc.scalar.copy(out=dst, in_=src)
+            else:
+                nc.vector.tensor_copy(out=dst, in_=src)
+
+        def kv_transposes(g):
+            n = groups[g][1]
+            bank = tp.tile([P, n, P], BF16, tag="tp", name="kvT_ps")
+            for j in range(n):
+                nc.tensor.transpose(bank[:, j, :], kv_in[g][:, j, :], ident_b[:])
+            banks[("kv", g)] = bank
+
+        def kv_copy(g):
+            nc.vector.tensor_copy(out=kvT[g][:], in_=banks[("kv", g)][:])
+
+        def d_transpose():
+            bank = tp.tile([P, QD], BF16, tag="tp", name="dT_ps")
+            nc.tensor.transpose(bank[:], d_in[:], ident_b[:])
+            banks["d"] = bank
+
+        def d_copy():
+            nc.vector.tensor_copy(out=dT[:], in_=banks["d"][:])
+
+        def bias_matmul():
+            bank = tp.tile([P, QD], F32, tag="tp", name="b_ps")
+            nc.tensor.matmul(out=bank[:], lhsT=ones_b[:], rhs=brow[:], start=True, stop=True)
+            banks["b"] = bank
+
+        def bias_copy(j):
+            nc.vector.tensor_copy(out=b4[:, j, :], in_=banks["b"][:])
+
+        def g_matmuls(g):
+            n = groups[g][1]
+            bank = gp.tile([P, n, QD], F32, tag="g", name="g_ps")
+            for j in range(n):
+                nc.tensor.matmul(out=bank[:, j, :], lhsT=kvT[g][:, j, :], rhs=dT[:], start=True, stop=True)
+            banks[("g", g)] = bank
+
+        def w_quantize():
+            nc.vector.quantize_mx(out=w_codes[:].bitcast(FP8X4), scales=w_scales[:], in_=w_grouped[:])
+
+        def x_transposes(i, h):
+            transpose_half(("x", i, h), x_in[i][h][:].bitcast(F32))
+
+        def x_copy(i, h):
+            if h == 0:
+                grouped[i] = work.tile([P, E], BF16, tag="grouped", name="grouped", bufs=4, align_bytes=64)
+            copy_half(("x", i, h), grouped[i], h, True)
+
+        def x_quantize(i):
+            codes[i] = const.tile([P, E // 4], U32, name="codes%d" % i, align_bytes=64)
+            scales[i] = const.tile([P, E // 4], U8, name="scales%d" % i, align_bytes=64)
+            nc.vector.quantize_mx(out=codes[i][:].bitcast(FP8X4), scales=scales[i][:], in_=grouped[i][:])
+
+        def x_matmuls(i):
+            g, j = tiles[i]
+            if j == 0:
+                q_ps[g] = qp.tile([P, groups[g][1], QD], F32, tag="q", name="q_ps")
+            for c in range(PASSES):
+                cols = slice(c * P, (c + 1) * P)
+                nc.tensor.matmul_mx(
+                    out=q_ps[g][:, j, :],
+                    lhsT=codes[i][:, cols].bitcast(FP8X4),
+                    lhsT_scale=scales[i][:, cols],
+                    rhs=w_codes[:, cols].bitcast(FP8X4),
+                    rhs_scale=w_scales[:, cols],
+                    start=(c == 0),
+                    stop=(c == PASSES - 1),
+                )
+
+        def e_piece(g, j0, j1):
+            n = groups[g][1]
+            if j0 == 0:
+                ep[("t", g)] = work.tile([P, n, QD], F32, tag="t", name="t")
+                ep[("y", g)] = work.tile([P, n, QD], F32, tag="y", name="y")
+                ep[("sums", g)] = []
+            t = ep[("t", g)]
+            y = ep[("y", g)]
+            sums = work.tile([P, 2], F32, tag="sums", name="sums", bufs=6)
+            junk = work.tile([P, j1 - j0, QD], F32, tag="junk", name="junk")
+            nc.vector.tensor_tensor(out=t[:, j0:j1, :], in0=q_ps[g][:, j0:j1, :], in1=b4[:, j0:j1, :], op=ALU.add)
+            nc.vector.scalar_tensor_tensor(
+                out=y[:, j0:j1, :], in0=t[:, j0:j1, :], scalar=1.0, in1=banks[("g", g)][:, j0:j1, :],
+                op0=ALU.mult, op1=ALU.mult, accum_out=sums[:, 0:1],
+            )
+            nc.scalar.activation(out=junk[:], in_=y[:, j0:j1, :], func=ACT.Square, accum_out=sums[:, 1:2])
+            ep[("sums", g)].append(sums)
+
+        def e_totals(g):
+            n = groups[g][1]
+            tot = tp.tile([P, 2], F32, tag="tp", name="tot")
+            parts = ep[("sums", g)]
+            for k, sums in enumerate(parts):
+                nc.tensor.matmul(out=tot[:], lhsT=sum_mask[n][:], rhs=sums[:], start=(k == 0), stop=(k == len(parts) - 1))
+            ep[("tot", g)] = tot
+
+        def e_moments(g):
+            mom = work.tile([P, 2], F32, tag="mom", name="mom")
+            nc.vector.tensor_scalar(out=mom[:], in0=ep[("tot", g)][:], scalar1=1.0 / (L * QD), scalar2=None, op0=ALU.mult)
+            ep[("mom", g)] = mom
+
+        def e_negvar(g):
+            mom = ep[("mom", g)]
+            negvar = work.tile([P, 1], F32, tag="negvar", name="negvar")
+            nc.vector.scalar_tensor_tensor(
+                out=negvar[:], in0=mom[:, 0:1], scalar=mom[:, 0:1], in1=mom[:, 1:2], op0=ALU.mult, op1=ALU.subtract
+            )
+            ep[("negvar", g)] = negvar
+
+        def e_std(g):
+            std = work.tile([P, 1], F32, tag="std", name="std")
+            nc.scalar.activation(out=std[:], in_=ep[("negvar", g)][:], func=ACT.Sqrt, bias=eps_col[:], scale=-1.0)
+            ep[("std", g)] = std
+
+        def e_rstd(g):
+            rstd = work.tile([P, 1], F32, tag="rstd", name="rstd")
+            nc.vector.reciprocal(out=rstd[:], in_=ep[("std", g)][:])
+            ep[("rstd", g)] = rstd
+
+        def e_normalise(g):
+            n = groups[g][1]
+            res = work.tile([P, n, QD], F32, tag="res", name="res")
+            nc.vector.tensor_scalar(
+                out=res[:], in0=ep[("y", g)][:], scalar1=ep[("mom", g)][:, 0:1], scalar2=ep[("rstd", g)][:],
+                op0=ALU.subtract, op1=ALU.mult,
+            )
+            ep[("res", g)] = res
+
+        def e_store0(g):
+            r0, n, i0 = groups[g]
+            nc.sync.dma_start(
+                out=o0_rows[r0 : r0 + P * n, :].rearrange("(p j) q -> p j q", j=n), in_=ep[("res", g)][:]
+            )
+
+        def e_amax(g):
+            n = groups[g][1]
+            amax = work.tile([P, n], F32, tag="amax", name="amax")
+            nc.vector.tensor_reduce(out=amax[:], in_=ep[("res", g)][:], axis=AXIS.X, op=ALU.max, apply_absolute_value=True)
+            ep[("amax", g)] = amax
+
+        def e_recip(g):
+            n = groups[g][1]
+            ramax = work.tile([P, n], F32, tag="ramax", name="ramax")
+            nc.vector.reciprocal(out=ramax[:], in_=ep[("amax", g)][:])
+            ep[("ramax", g)] = ramax
+
+        def e_factor(g):
+            n = groups[g][1]
+            factor = work.tile([P, n], F32, tag="factor", name="factor")
+            nc.vector.tensor_scalar(out=factor[:], in0=ep[("ramax", g)][:], scalar1=448.0, scalar2=None, op0=ALU.mult)
+            ep[("factor", g)] = factor
+
+        def e_cast(g, j):
+            n = groups[g][1]
+            if j == 0:
+                ep[("o8", g)] = work.tile([P, n, QD], FP8, tag="o8", name="o8")
+            o8 = ep[("o8", g)]
+            res = ep[("res", g)]
+            factor = ep[("factor", g)]
+            if j in SCALAR_CASTS:
+                nc.scalar.activation(
+                    out=o8[:, j, :], in_=res[:, j, :], func=ACT.Identity, bias=zero_col[:], scale=factor[:, j : j + 1],
+                    saturate=False,
+                )
+            else:
+                nc.vector.tensor_scalar(
+                    out=o8[:, j, :], in0=res[:, j, :], scalar1=factor[:, j : j + 1], scalar2=None, op0=ALU.mult,
+                    saturate=False,
+                )
+
+        def e_store1(g):
+            r0, n, i0 = groups[g]
+            nc.sync.dma_start(
+                out=o1_rows[r0 : r0 + P * n, :].rearrange("(p j) q -> p (j q)", j=n),
+                in_=ep[("o8", g)][:].bitcast(U8).rearrange("p j q -> p (j q)"),
+            )
+
+        def tile_in(i):
+            for h in range(2):
+                x_transposes(i, h)
+                x_copy(i, h)
+            x_quantize(i)
+
+        def kv_in_turn(g):
+            kv_transposes(g)
+            kv_copy(g)
+
+        def finish(pending):
+            for g in pending:
+                e_totals(g)
+            for g in pending:
+                e_moments(g)
+                e_negvar(g)
+                e_std(g)
+                e_rstd(g)
+                e_normalise(g)
+                e_store0(g)
+                e_amax(g)
+                e_recip(g)
+                e_factor(g)
+                for j in range(groups[g][1]):
+                    e_cast(g, j)
+                e_store1(g)
+
+        def bring(i):
+            if i in first_of:
+                kv_in_turn(first_of[i])
+            tile_in(i)
+
+        first_of = dict((i0, g) for g, (r0, n, i0) in enumerate(groups))
+        last_of = dict((i0 + n - 1, g) for g, (r0, n, i0) in enumerate(groups))
+
+        load_order = [("x", 0), ("x", 1), ("w", 0), ("w", 1), ("kv", 0), ("d", 0), ("b", 0)]
+        for i in range(2, n_tiles):
+            if i in first_of:
+                load_order.append(("kv", first_of[i]))
+            load_order.append(("x", i))
+
+        with tc.manual_schedule(engines={mybir.EngineType.PE, mybir.EngineType.SP}):
+            for what, k in load_order:
+                if what == "x":
+                    g, j = tiles[k]
+                    r0, n, i0 = groups[g]
+                    rows = x_rows[r0 : r0 + P * n, :].rearrange("(p j) e -> p j e", j=n)
+                    for h in range(2):
+                        nc.sync.dma_start(out=x_in[k][h][:], in_=rows[:, j, (E // 2) * h : (E // 2) * (h + 1)])
+                elif what == "w":
+                    nc.sync.dma_start(out=w_in[k][:], in_=Wq[:, (E // 2) * k : (E // 2) * (k + 1)])
+                elif what == "kv":
+                    r0, n, i0 = groups[k]
+                    nc.sync.dma_start(out=kv_in[k][:], in_=kv_rows[r0 : r0 + P * n, :].rearrange("(p j) k -> p j k", j=n))
+                elif what == "d":
+                    nc.sync.dma_start(out=d_in[:], in_=decay_mask.rearrange("o j i -> (o j) i"))
+                else:
+                    nc.sync.dma_start(out=brow[0:1, :], in_=bq.rearrange("(o q) -> o q", o=1))
+
+            tile_in(0)
+            tile_in(1)
+            for h in range(2):
+                transpose_half(("w", h), w_in[h][:].bitcast(F32))
+                copy_half(("w", h), w_grouped, h, True)
+            w_quantize()
+            kv_in_turn(0)
+            d_transpose()
+            d_copy()
+            bias_matmul()
+            for j in range(4):
+                bias_copy(j)
+            for i in range(2, 2 * RUN):
+                bring(i)
+
+            waiting = []
+            for first in range(0, n_tiles, RUN):
+                run = range(first, first + RUN)
+                for i in run:
+                    if i in first_of:
+                        g_matmuls(first_of[i])
+                j0 = -1
+                for i in run:
+                    g, j = tiles[i]
+                    x_matmuls(i)
+                    if j0 < 0:
+                        j0 = j
+                    if i in last_of or i == first + RUN - 1:
+                        e_piece(g, j0, j + 1)
+                        j0 = -1
+                finish(waiting)
+                waiting = [last_of[i] for i in run if i in last_of]
+                for i in range(first + 2 * RUN, min(first + 3 * RUN, n_tiles)):
+                    bring(i)
+            finish(waiting)

@@ -19,7 +19,7 @@ P = 128
 PASSES = E // (4 * P)
 FLOPS = 2 * B * L * E * QD + 2 * B * L * L * QD
 
-GROUPS = (4, 4, 4, 4)
+GROUPS = (4, 4, 4, 2, 2)
 RUN = 2
 SCALAR_CASTS = (1, 3)
 
@@ -43,7 +43,7 @@ def tile_parallelretention_pb_kernel(tc, x, Wq, bq, kv, decay_mask, out_0, out_1
     with ExitStack() as ctx:
         const = ctx.enter_context(tc.tile_pool(name="const", bufs=1))
         xin = ctx.enter_context(tc.tile_pool(name="xin", bufs=1))
-        work = ctx.enter_context(tc.tile_pool(name="work", bufs=2))
+        work = ctx.enter_context(tc.tile_pool(name="work", bufs=3))
         tp = ctx.enter_context(tc.psum_pool(name="tp", bufs=5))
         gp = ctx.enter_context(tc.psum_pool(name="gp", bufs=1))
         qp = ctx.enter_context(tc.psum_pool(name="qp", bufs=2))
@@ -53,13 +53,11 @@ def tile_parallelretention_pb_kernel(tc, x, Wq, bq, kv, decay_mask, out_0, out_1
         ones_b = const.tile([P, P], BF16, name="ones_b")
         brow = const.tile([P, QD], BF16, name="brow")
         zero_col = const.tile([P, 1], F32, name="zero_col")
-        eps_col = const.tile([P, 1], F32, name="eps_col")
         warm = const.tile([P, 1], F32, name="warm")
         nc.vector.memset(brow[:], 0.0)
-        nc.vector.memset(eps_col[:], EPS)
         nc.vector.memset(ones_b[:], 1.0)
         nc.vector.memset(zero_col[:], 0.0)
-        nc.scalar.activation(out=warm[:], in_=eps_col[:], func=ACT.Sqrt)
+        nc.scalar.activation(out=warm[:], in_=zero_col[:], func=ACT.Sqrt)
         make_identity(nc, ident_b[:])
         make_identity(nc, ident_f[:])
         sum_mask = {}
@@ -70,7 +68,9 @@ def tile_parallelretention_pb_kernel(tc, x, Wq, bq, kv, decay_mask, out_0, out_1
                     nc.vector.memset(blockdiag[:], 1.0)
                 else:
                     make_block_diagonal(nc, blockdiag[:], P // n)
-                sum_mask[n] = blockdiag
+                mean_mask = const.tile([P, P], F32, name="mean_mask%d" % n)
+                nc.vector.tensor_scalar(out=mean_mask[:], in0=blockdiag[:], scalar1=1.0 / (L * QD), scalar2=None, op0=ALU.mult)
+                sum_mask[n] = mean_mask
 
         d_in = xin.tile([P, L], BF16, name="d_in")
         kv_in = [xin.tile([P, n, L], BF16, name="kv_in%d" % g) for g, (r0, n, i0) in enumerate(groups)]
@@ -131,12 +131,12 @@ def tile_parallelretention_pb_kernel(tc, x, Wq, bq, kv, decay_mask, out_0, out_1
         def bias_copy(j):
             nc.vector.tensor_copy(out=b4[:, j, :], in_=banks["b"][:])
 
-        def g_matmuls(g):
-            n = groups[g][1]
-            bank = gp.tile([P, n, QD], F32, tag="g", name="g_ps")
-            for j in range(n):
-                nc.tensor.matmul(out=bank[:, j, :], lhsT=kvT[g][:, j, :], rhs=dT[:], start=True, stop=True)
-            banks[("g", g)] = bank
+        def g_matmuls(b):
+            bank = gp.tile([P, 4, QD], F32, tag="g", name="g_ps")
+            for s in range(4):
+                g, j = tiles[4 * b + s]
+                nc.tensor.matmul(out=bank[:, s, :], lhsT=kvT[g][:, j, :], rhs=dT[:], start=True, stop=True)
+            banks[("g", b)] = bank
 
         def w_quantize():
             nc.vector.quantize_mx(out=w_codes[:].bitcast(FP8X4), scales=w_scales[:], in_=w_grouped[:])
@@ -153,6 +153,28 @@ def tile_parallelretention_pb_kernel(tc, x, Wq, bq, kv, decay_mask, out_0, out_1
             codes[i] = const.tile([P, E // 4], U32, name="codes%d" % i, align_bytes=64)
             scales[i] = const.tile([P, E // 4], U8, name="scales%d" % i, align_bytes=64)
             nc.vector.quantize_mx(out=codes[i][:].bitcast(FP8X4), scales=scales[i][:], in_=grouped[i][:])
+
+        def x_transposes_pass(i, c):
+            words = x_in[i][c // 2][:].bitcast(F32)
+            bank = tp.tile([P, 2, P], F32, tag="tp", name="xT_pass")
+            for u in range(2):
+                nc.tensor.transpose(bank[:, u, :], words[:, 256 * (c % 2) + u : 256 * (c % 2 + 1) : 2], ident_f[:])
+            banks[("xp", i, c)] = bank
+
+        def x_copy_pass(i, c):
+            if c == 0:
+                grouped[i] = work.tile([P, E], BF16, tag="grouped", name="grouped", bufs=4, align_bytes=64)
+            dst = grouped[i][:].bitcast(F32)[:, 256 * c : 256 * (c + 1)].rearrange("p (r u) -> p r u", u=2)
+            nc.scalar.copy(out=dst, in_=banks[("xp", i, c)][:].rearrange("p u r -> p r u"))
+
+        def x_quantize_pass(i, c):
+            if c == 0:
+                codes[i] = const.tile([P, E // 4], U32, name="codes%d" % i, align_bytes=64)
+                scales[i] = const.tile([P, E // 4], U8, name="scales%d" % i, align_bytes=64)
+            cols = slice(c * P, (c + 1) * P)
+            nc.vector.quantize_mx(
+                out=codes[i][:, cols].bitcast(FP8X4), scales=scales[i][:, cols], in_=grouped[i][:, 4 * P * c : 4 * P * (c + 1)]
+            )
 
         def x_matmuls(i):
             g, j = tiles[i]
@@ -171,7 +193,7 @@ def tile_parallelretention_pb_kernel(tc, x, Wq, bq, kv, decay_mask, out_0, out_1
                 )
 
         def e_piece(g, j0, j1):
-            n = groups[g][1]
+            r0, n, i0 = groups[g]
             if j0 == 0:
                 ep[("t", g)] = work.tile([P, n, QD], F32, tag="t", name="t")
                 ep[("y", g)] = work.tile([P, n, QD], F32, tag="y", name="y")
@@ -182,11 +204,12 @@ def tile_parallelretention_pb_kernel(tc, x, Wq, bq, kv, decay_mask, out_0, out_1
             junk = work.tile([P, j1 - j0, QD], F32, tag="junk", name="junk")
             nc.vector.tensor_tensor(out=t[:, j0:j1, :], in0=q_ps[g][:, j0:j1, :], in1=b4[:, j0:j1, :], op=ALU.add)
             nc.vector.scalar_tensor_tensor(
-                out=y[:, j0:j1, :], in0=t[:, j0:j1, :], scalar=1.0, in1=banks[("g", g)][:, j0:j1, :],
+                out=y[:, j0:j1, :], in0=t[:, j0:j1, :], scalar=1.0, in1=banks[("g", i0 // 4)][:, i0 % 4 + j0 : i0 % 4 + j1, :],
                 op0=ALU.mult, op1=ALU.mult, accum_out=sums[:, 0:1],
             )
             nc.scalar.activation(out=junk[:], in_=y[:, j0:j1, :], func=ACT.Square, accum_out=sums[:, 1:2])
             ep[("sums", g)].append(sums)
+
 
         def e_totals(g):
             n = groups[g][1]
@@ -198,20 +221,15 @@ def tile_parallelretention_pb_kernel(tc, x, Wq, bq, kv, decay_mask, out_0, out_1
 
         def e_moments(g):
             mom = work.tile([P, 2], F32, tag="mom", name="mom")
-            nc.vector.tensor_scalar(out=mom[:], in0=ep[("tot", g)][:], scalar1=1.0 / (L * QD), scalar2=None, op0=ALU.mult)
+            tot = ep[("tot", g)]
+            nc.vector.tensor_scalar(out=mom[:, 0:1], in0=tot[:, 0:1], scalar1=-1.0, scalar2=None, op0=ALU.mult)
+            nc.vector.tensor_scalar(out=mom[:, 1:2], in0=tot[:, 1:2], scalar1=EPS, scalar2=None, op0=ALU.add)
             ep[("mom", g)] = mom
-
-        def e_negvar(g):
-            mom = ep[("mom", g)]
-            negvar = work.tile([P, 1], F32, tag="negvar", name="negvar")
-            nc.vector.scalar_tensor_tensor(
-                out=negvar[:], in0=mom[:, 0:1], scalar=mom[:, 0:1], in1=mom[:, 1:2], op0=ALU.mult, op1=ALU.subtract
-            )
-            ep[("negvar", g)] = negvar
 
         def e_std(g):
             std = work.tile([P, 1], F32, tag="std", name="std")
-            nc.scalar.activation(out=std[:], in_=ep[("negvar", g)][:], func=ACT.Sqrt, bias=eps_col[:], scale=-1.0)
+            mom = ep[("mom", g)]
+            nc.scalar.activation(out=std[:], in_=ep[("tot", g)][:, 0:1], func=ACT.Sqrt, bias=mom[:, 1:2], scale=mom[:, 0:1])
             ep[("std", g)] = std
 
         def e_rstd(g):
@@ -224,7 +242,7 @@ def tile_parallelretention_pb_kernel(tc, x, Wq, bq, kv, decay_mask, out_0, out_1
             res = work.tile([P, n, QD], F32, tag="res", name="res")
             nc.vector.tensor_scalar(
                 out=res[:], in0=ep[("y", g)][:], scalar1=ep[("mom", g)][:, 0:1], scalar2=ep[("rstd", g)][:],
-                op0=ALU.subtract, op1=ALU.mult,
+                op0=ALU.add, op1=ALU.mult,
             )
             ep[("res", g)] = res
 
@@ -250,6 +268,33 @@ def tile_parallelretention_pb_kernel(tc, x, Wq, bq, kv, decay_mask, out_0, out_1
             n = groups[g][1]
             factor = work.tile([P, n], F32, tag="factor", name="factor")
             nc.vector.tensor_scalar(out=factor[:], in0=ep[("ramax", g)][:], scalar1=448.0, scalar2=None, op0=ALU.mult)
+            ep[("factor", g)] = factor
+
+        def e_extremes(g):
+            n = groups[g][1]
+            ext = work.tile([P, 2, n], F32, tag="ext", name="ext")
+            nc.vector.tensor_reduce(out=ext[:, 0, :], in_=ep[("y", g)][:], axis=AXIS.X, op=ALU.max)
+            nc.vector.tensor_reduce(out=ext[:, 1, :], in_=ep[("y", g)][:], axis=AXIS.X, op=ALU.min)
+            ep[("ext", g)] = ext
+
+        def e_spread(g):
+            n = groups[g][1]
+            dev = work.tile([P, 2, n], F32, tag="dev", name="dev")
+            spread = work.tile([P, n], F32, tag="spread", name="spread")
+            rspread = work.tile([P, n], F32, tag="rspread", name="rspread")
+            nc.vector.tensor_scalar(out=dev[:], in0=ep[("ext", g)][:], scalar1=ep[("mom", g)][:, 0:1], scalar2=None, op0=ALU.add)
+            nc.vector.scalar_tensor_tensor(
+                out=spread[:], in0=dev[:, 1, :], scalar=-1.0, in1=dev[:, 0, :], op0=ALU.mult, op1=ALU.max
+            )
+            nc.vector.reciprocal(out=rspread[:], in_=spread[:])
+            ep[("rspread", g)] = rspread
+
+        def e_factor_from_spread(g):
+            n = groups[g][1]
+            factor = work.tile([P, n], F32, tag="factor", name="factor")
+            nc.vector.tensor_scalar(
+                out=factor[:], in0=ep[("rspread", g)][:], scalar1=ep[("std", g)][:], scalar2=448.0, op0=ALU.mult, op1=ALU.mult
+            )
             ep[("factor", g)] = factor
 
         def e_cast(g, j):
@@ -278,6 +323,12 @@ def tile_parallelretention_pb_kernel(tc, x, Wq, bq, kv, decay_mask, out_0, out_1
             )
 
         def tile_in(i):
+            if i == n_tiles - 1:
+                for c in range(PASSES):
+                    x_transposes_pass(i, c)
+                    x_copy_pass(i, c)
+                    x_quantize_pass(i, c)
+                return
             for h in range(2):
                 x_transposes(i, h)
                 x_copy(i, h)
@@ -291,15 +342,21 @@ def tile_parallelretention_pb_kernel(tc, x, Wq, bq, kv, decay_mask, out_0, out_1
             for g in pending:
                 e_totals(g)
             for g in pending:
+                if g == len(groups) - 1:
+                    e_extremes(g)
                 e_moments(g)
-                e_negvar(g)
                 e_std(g)
+                if g == len(groups) - 1:
+                    e_spread(g)
                 e_rstd(g)
                 e_normalise(g)
                 e_store0(g)
-                e_amax(g)
-                e_recip(g)
-                e_factor(g)
+                if g == len(groups) - 1:
+                    e_factor_from_spread(g)
+                else:
+                    e_amax(g)
+                    e_recip(g)
+                    e_factor(g)
                 for j in range(groups[g][1]):
                     e_cast(g, j)
                 e_store1(g)
@@ -355,15 +412,15 @@ def tile_parallelretention_pb_kernel(tc, x, Wq, bq, kv, decay_mask, out_0, out_1
             for first in range(0, n_tiles, RUN):
                 run = range(first, first + RUN)
                 for i in run:
-                    if i in first_of:
-                        g_matmuls(first_of[i])
+                    if i % 4 == 0:
+                        g_matmuls(i // 4)
                 j0 = -1
                 for i in run:
                     g, j = tiles[i]
                     x_matmuls(i)
                     if j0 < 0:
                         j0 = j
-                    if i in last_of or i == first + RUN - 1:
+                    if i in last_of or i == first + RUN - 1 or g == len(groups) - 1:
                         e_piece(g, j0, j + 1)
                         j0 = -1
                 finish(waiting)

@@ -131,12 +131,11 @@ def tile_parallelretention_pb_kernel(tc, x, Wq, bq, kv, decay_mask, out_0, out_1
         def bias_copy(j):
             nc.vector.tensor_copy(out=b4[:, j, :], in_=banks["b"][:])
 
-        def g_matmuls(b):
-            bank = gp.tile([P, 4, QD], F32, tag="g", name="g_ps")
-            for s in range(4):
-                g, j = tiles[4 * b + s]
-                nc.tensor.matmul(out=bank[:, s, :], lhsT=kvT[g][:, j, :], rhs=dT[:], start=True, stop=True)
-            banks[("g", b)] = bank
+        def g_matmul(i):
+            if i % 4 == 0:
+                banks[("g", i // 4)] = gp.tile([P, 4, QD], F32, tag="g", name="g_ps")
+            g, j = tiles[i]
+            nc.tensor.matmul(out=banks[("g", i // 4)][:, i % 4, :], lhsT=kvT[g][:, j, :], rhs=dT[:], start=True, stop=True)
 
         def w_quantize():
             nc.vector.quantize_mx(out=w_codes[:].bitcast(FP8X4), scales=w_scales[:], in_=w_grouped[:])
@@ -411,18 +410,22 @@ def tile_parallelretention_pb_kernel(tc, x, Wq, bq, kv, decay_mask, out_0, out_1
             waiting = []
             for first in range(0, n_tiles, RUN):
                 run = range(first, first + RUN)
-                for i in run:
-                    if i % 4 == 0:
-                        g_matmuls(i // 4)
-                j0 = -1
+                last_run = first + RUN == n_tiles
+                if not last_run:
+                    g_matmul(first)
                 for i in run:
                     g, j = tiles[i]
                     x_matmuls(i)
-                    if j0 < 0:
-                        j0 = j
-                    if i in last_of or i == first + RUN - 1 or g == len(groups) - 1:
-                        e_piece(g, j0, j + 1)
-                        j0 = -1
+                    if last_run:
+                        e_piece(g, j, j + 1)
+                if not last_run:
+                    g_matmul(first + 1)
+                    if first + 2 * RUN == n_tiles:
+                        g_matmul(first + 2)
+                        g_matmul(first + 3)
+                    if first + 1 in last_of:
+                        g, j = tiles[first + 1]
+                        e_piece(g, 0, j + 1)
                 finish(waiting)
                 waiting = [last_of[i] for i in run if i in last_of]
                 for i in range(first + 2 * RUN, min(first + 3 * RUN, n_tiles)):

@@ -45,8 +45,8 @@ def tile_parallelretention_pb_kernel(tc, x, Wq, bq, kv, decay_mask, out_0, out_1
         xin = ctx.enter_context(tc.tile_pool(name="xin", bufs=1))
         work = ctx.enter_context(tc.tile_pool(name="work", bufs=3))
         tp = ctx.enter_context(tc.psum_pool(name="tp", bufs=5))
-        gp = ctx.enter_context(tc.psum_pool(name="gp", bufs=1))
-        qp = ctx.enter_context(tc.psum_pool(name="qp", bufs=2))
+        gp = ctx.enter_context(tc.psum_pool(name="gp", bufs=2))
+        qp = ctx.enter_context(tc.psum_pool(name="qp", bufs=1))
 
         ident_b = const.tile([P, P], BF16, name="ident_b")
         ident_f = const.tile([P, P], F32, name="ident_f")
@@ -361,8 +361,10 @@ def tile_parallelretention_pb_kernel(tc, x, Wq, bq, kv, decay_mask, out_0, out_1
                 e_store1(g)
 
         def bring(i):
-            if i in first_of:
-                kv_in_turn(first_of[i])
+            if i % 4 == 0:
+                for k in range(i, i + 4):
+                    if k in first_of:
+                        kv_in_turn(first_of[k])
             tile_in(i)
 
         first_of = dict((i0, g) for g, (r0, n, i0) in enumerate(groups))
@@ -370,8 +372,10 @@ def tile_parallelretention_pb_kernel(tc, x, Wq, bq, kv, decay_mask, out_0, out_1
 
         load_order = [("x", 0), ("x", 1), ("w", 0), ("w", 1), ("kv", 0), ("d", 0), ("b", 0)]
         for i in range(2, n_tiles):
-            if i in first_of:
-                load_order.append(("kv", first_of[i]))
+            if i % 4 == 0:
+                for k in range(i, i + 4):
+                    if k in first_of:
+                        load_order.append(("kv", first_of[k]))
             load_order.append(("x", i))
 
         with tc.manual_schedule(engines={mybir.EngineType.PE, mybir.EngineType.SP}):
@@ -404,30 +408,28 @@ def tile_parallelretention_pb_kernel(tc, x, Wq, bq, kv, decay_mask, out_0, out_1
             bias_matmul()
             for j in range(4):
                 bias_copy(j)
-            for i in range(2, 2 * RUN):
-                bring(i)
+            bring(2)
+            g_matmul(0)
+            g_matmul(1)
+            bring(3)
 
             waiting = []
             for first in range(0, n_tiles, RUN):
                 run = range(first, first + RUN)
                 last_run = first + RUN == n_tiles
-                if not last_run:
-                    g_matmul(first)
                 for i in run:
                     g, j = tiles[i]
                     x_matmuls(i)
                     if last_run:
                         e_piece(g, j, j + 1)
-                if not last_run:
-                    g_matmul(first + 1)
-                    if first + 2 * RUN == n_tiles:
-                        g_matmul(first + 2)
-                        g_matmul(first + 3)
-                    if first + 1 in last_of:
-                        g, j = tiles[first + 1]
-                        e_piece(g, 0, j + 1)
+                if not last_run and first + 1 in last_of:
+                    g, j = tiles[first + 1]
+                    e_piece(g, 0, j + 1)
                 finish(waiting)
                 waiting = [last_of[i] for i in run if i in last_of]
-                for i in range(first + 2 * RUN, min(first + 3 * RUN, n_tiles)):
-                    bring(i)
+                if first + 2 * RUN < n_tiles:
+                    bring(first + 2 * RUN)
+                    for i in range(first + RUN, first + (3 if first + 3 * RUN == n_tiles else 2) * RUN):
+                        g_matmul(i)
+                    bring(first + 2 * RUN + 1)
             finish(waiting)

@@ -58,8 +58,8 @@ def tile_parallelretention_pb_kernel(tc, x, Wq, bq, kv, decay_mask, out_0, out_1
         nc.vector.memset(ones_b[:], 1.0)
         nc.vector.memset(zero_col[:], 0.0)
         nc.scalar.activation(out=warm[:], in_=zero_col[:], func=ACT.Sqrt)
-        make_identity(nc, ident_b[:])
         make_identity(nc, ident_f[:])
+        make_identity(nc, ident_b[:])
         sum_mask = {}
         for n in GROUPS:
             if n not in sum_mask:
@@ -177,7 +177,9 @@ def tile_parallelretention_pb_kernel(tc, x, Wq, bq, kv, decay_mask, out_0, out_1
 
         def x_matmuls(i):
             g, j = tiles[i]
-            if j == 0:
+            if j == 0 and g == len(groups) - 1:
+                q_ps[g] = tp.tile([P, groups[g][1], QD], F32, tag="tp", name="q_last")
+            elif j == 0:
                 q_ps[g] = qp.tile([P, groups[g][1], QD], F32, tag="q", name="q_ps")
             for c in range(PASSES):
                 cols = slice(c * P, (c + 1) * P)

@@ -22,6 +22,7 @@ FLOPS = 2 * B * L * E * QD + 2 * B * L * L * QD
 GROUPS = (4, 4, 4, 2, 2)
 RUN = 2
 SCALAR_CASTS = (1, 3)
+WHOLE_FROM = 4
 
 
 def tile_parallelretention_pb_kernel(tc, x, Wq, bq, kv, decay_mask, out_0, out_1):
@@ -75,7 +76,18 @@ def tile_parallelretention_pb_kernel(tc, x, Wq, bq, kv, decay_mask, out_0, out_1
         d_in = xin.tile([P, L], BF16, name="d_in")
         kv_in = [xin.tile([P, n, L], BF16, name="kv_in%d" % g) for g, (r0, n, i0) in enumerate(groups)]
         w_in = [xin.tile([P, E // 2], BF16, name="w_in%d" % h) for h in range(2)]
-        x_in = [[xin.tile([P, E // 2], BF16, name="x_in%d_%d" % (i, h)) for h in range(2)] for i in range(n_tiles)]
+        x_in = [
+            [xin.tile([P, E // 2], BF16, name="x_in%d_%d" % (i, h)) for h in range(2)]
+            if i < WHOLE_FROM
+            else [xin.tile([P, E], BF16, name="x_in%d" % i)]
+            for i in range(n_tiles)
+        ]
+
+        def x_words(i, h):
+            if i < WHOLE_FROM:
+                return x_in[i][h][:].bitcast(F32)
+            return x_in[i][0][:, (E // 2) * h : (E // 2) * (h + 1)].bitcast(F32)
+
         kvT = [const.tile([P, n, P], BF16, name="kvT%d" % g) for g, (r0, n, i0) in enumerate(groups)]
         dT = const.tile([P, QD], BF16, name="dT")
         b4 = const.tile([P, 4, QD], F32, name="b4")
@@ -141,7 +153,7 @@ def tile_parallelretention_pb_kernel(tc, x, Wq, bq, kv, decay_mask, out_0, out_1
             nc.vector.quantize_mx(out=w_codes[:].bitcast(FP8X4), scales=w_scales[:], in_=w_grouped[:])
 
         def x_transposes(i, h):
-            transpose_half(("x", i, h), x_in[i][h][:].bitcast(F32))
+            transpose_half(("x", i, h), x_words(i, h))
 
         def x_copy(i, h):
             if h == 0:
@@ -154,7 +166,7 @@ def tile_parallelretention_pb_kernel(tc, x, Wq, bq, kv, decay_mask, out_0, out_1
             nc.vector.quantize_mx(out=codes[i][:].bitcast(FP8X4), scales=scales[i][:], in_=grouped[i][:])
 
         def x_transposes_pass(i, c):
-            words = x_in[i][c // 2][:].bitcast(F32)
+            words = x_words(i, c // 2)
             bank = tp.tile([P, 2, P], F32, tag="tp", name="xT_pass")
             for u in range(2):
                 nc.tensor.transpose(bank[:, u, :], words[:, 256 * (c % 2) + u : 256 * (c % 2 + 1) : 2], ident_f[:])
@@ -386,8 +398,11 @@ def tile_parallelretention_pb_kernel(tc, x, Wq, bq, kv, decay_mask, out_0, out_1
                     g, j = tiles[k]
                     r0, n, i0 = groups[g]
                     rows = x_rows[r0 : r0 + P * n, :].rearrange("(p j) e -> p j e", j=n)
-                    for h in range(2):
-                        nc.sync.dma_start(out=x_in[k][h][:], in_=rows[:, j, (E // 2) * h : (E // 2) * (h + 1)])
+                    if k < WHOLE_FROM:
+                        for h in range(2):
+                            nc.sync.dma_start(out=x_in[k][h][:], in_=rows[:, j, (E // 2) * h : (E // 2) * (h + 1)])
+                    else:
+                        nc.sync.dma_start(out=x_in[k][0][:], in_=rows[:, j, :])
                 elif what == "w":
                     nc.sync.dma_start(out=w_in[k][:], in_=Wq[:, (E // 2) * k : (E // 2) * (k + 1)])
                 elif what == "kv":

@@ -19,10 +19,14 @@ P = 128
 PASSES = E // (4 * P)
 FLOPS = 2 * B * L * E * QD + 2 * B * L * L * QD
 
-GROUPS = (4, 4, 4, 2, 2)
-RUN = 2
-SCALAR_CASTS = (1, 3)
+GROUPS = (4, 4, 2, 2, 2, 2)
+LAST = len(GROUPS) - 1
+N_RUNS = B // 2
 WHOLE_FROM = 4
+SORTED = ()
+ACT_NORM = ()
+GPSIMD_NORM = ()
+ACT_CASTS = (1, 3)
 
 
 def tile_parallelretention_pb_kernel(tc, x, Wq, bq, kv, decay_mask, out_0, out_1):
@@ -54,21 +58,20 @@ def tile_parallelretention_pb_kernel(tc, x, Wq, bq, kv, decay_mask, out_0, out_1
         ones_b = const.tile([P, P], BF16, name="ones_b")
         brow = const.tile([P, QD], BF16, name="brow")
         zero_col = const.tile([P, 1], F32, name="zero_col")
+        one_col = const.tile([P, 1], F32, name="one_col")
         warm = const.tile([P, 1], F32, name="warm")
+        nc.vector.memset(one_col[:], 1.0)
         nc.vector.memset(brow[:], 0.0)
         nc.vector.memset(ones_b[:], 1.0)
         nc.vector.memset(zero_col[:], 0.0)
-        nc.scalar.activation(out=warm[:], in_=zero_col[:], func=ACT.Sqrt)
+        nc.scalar.activation(out=warm[:], in_=one_col[:], func=ACT.Abs_reciprocal_sqrt)
         make_identity(nc, ident_f[:])
         make_identity(nc, ident_b[:])
         sum_mask = {}
         for n in GROUPS:
             if n not in sum_mask:
                 blockdiag = const.tile([P, P], F32, name="blockdiag%d" % n)
-                if n == 1:
-                    nc.vector.memset(blockdiag[:], 1.0)
-                else:
-                    make_block_diagonal(nc, blockdiag[:], P // n)
+                make_block_diagonal(nc, blockdiag[:], P // n)
                 mean_mask = const.tile([P, P], F32, name="mean_mask%d" % n)
                 nc.vector.tensor_scalar(out=mean_mask[:], in0=blockdiag[:], scalar1=1.0 / (L * QD), scalar2=None, op0=ALU.mult)
                 sum_mask[n] = mean_mask
@@ -90,7 +93,7 @@ def tile_parallelretention_pb_kernel(tc, x, Wq, bq, kv, decay_mask, out_0, out_1
 
         kvT = [const.tile([P, n, P], BF16, name="kvT%d" % g) for g, (r0, n, i0) in enumerate(groups)]
         dT = const.tile([P, QD], BF16, name="dT")
-        b4 = const.tile([P, 4, QD], F32, name="b4")
+        b4 = const.tile([P, 2, QD], F32, name="b4")
         w_grouped = const.tile([P, E], BF16, name="w_grouped", align_bytes=64)
         w_codes = const.tile([P, E // 4], U32, name="w_codes", align_bytes=64)
         w_scales = const.tile([P, E // 4], U8, name="w_scales", align_bytes=64)
@@ -101,6 +104,7 @@ def tile_parallelretention_pb_kernel(tc, x, Wq, bq, kv, decay_mask, out_0, out_1
         scales = {}
         q_ps = {}
         ep = {}
+        sorted_words = {}
 
         def transpose_half(key, words):
             bank = tp.tile([P, 2, 2, P], F32, tag="tp", name="xT")
@@ -109,13 +113,16 @@ def tile_parallelretention_pb_kernel(tc, x, Wq, bq, kv, decay_mask, out_0, out_1
                     nc.tensor.transpose(bank[:, c, u, :], words[:, 256 * c + u : 256 * (c + 1) : 2], ident_f[:])
             banks[key] = bank
 
-        def copy_half(key, dst_tile, h, on_scalar):
+        def transpose_sorted_half(key, words):
+            bank = tp.tile([P, 2, 2, P], F32, tag="tp", name="xT")
+            for c in range(2):
+                for u in range(2):
+                    nc.tensor.transpose(bank[:, c, u, :], words[:, c, u, :], ident_f[:])
+            banks[key] = bank
+
+        def copy_half(key, dst_tile, h):
             dst = dst_tile[:].bitcast(F32)[:, 512 * h : 512 * (h + 1)].rearrange("p (c r u) -> p c r u", c=2, u=2)
-            src = banks[key][:].rearrange("p c u r -> p c r u")
-            if on_scalar:
-                nc.scalar.copy(out=dst, in_=src)
-            else:
-                nc.vector.tensor_copy(out=dst, in_=src)
+            nc.scalar.copy(out=dst, in_=banks[key][:].rearrange("p c u r -> p c r u"))
 
         def kv_transposes(g):
             n = groups[g][1]
@@ -152,13 +159,23 @@ def tile_parallelretention_pb_kernel(tc, x, Wq, bq, kv, decay_mask, out_0, out_1
         def w_quantize():
             nc.vector.quantize_mx(out=w_codes[:].bitcast(FP8X4), scales=w_scales[:], in_=w_grouped[:])
 
+        def x_sort(i, h):
+            if h == 0:
+                sorted_words[i] = work.tile([P, 2, 2, 2, P], F32, tag="sorted", name="sorted", bufs=2)
+            nc.vector.tensor_copy(
+                out=sorted_words[i][:, h, :, :, :], in_=x_words(i, h).rearrange("p (c r u) -> p c u r", c=2, u=2)
+            )
+
         def x_transposes(i, h):
-            transpose_half(("x", i, h), x_words(i, h))
+            if i in SORTED:
+                transpose_sorted_half(("x", i, h), sorted_words[i][:, h, :, :, :])
+            else:
+                transpose_half(("x", i, h), x_words(i, h))
 
         def x_copy(i, h):
             if h == 0:
                 grouped[i] = work.tile([P, E], BF16, tag="grouped", name="grouped", bufs=4, align_bytes=64)
-            copy_half(("x", i, h), grouped[i], h, True)
+            copy_half(("x", i, h), grouped[i], h)
 
         def x_quantize(i):
             codes[i] = const.tile([P, E // 4], U32, name="codes%d" % i, align_bytes=64)
@@ -187,16 +204,11 @@ def tile_parallelretention_pb_kernel(tc, x, Wq, bq, kv, decay_mask, out_0, out_1
                 out=codes[i][:, cols].bitcast(FP8X4), scales=scales[i][:, cols], in_=grouped[i][:, 4 * P * c : 4 * P * (c + 1)]
             )
 
-        def x_matmuls(i):
-            g, j = tiles[i]
-            if j == 0 and g == len(groups) - 1:
-                q_ps[g] = tp.tile([P, groups[g][1], QD], F32, tag="tp", name="q_last")
-            elif j == 0:
-                q_ps[g] = qp.tile([P, groups[g][1], QD], F32, tag="q", name="q_ps")
+        def x_matmuls(i, q):
             for c in range(PASSES):
                 cols = slice(c * P, (c + 1) * P)
                 nc.tensor.matmul_mx(
-                    out=q_ps[g][:, j, :],
+                    out=q,
                     lhsT=codes[i][:, cols].bitcast(FP8X4),
                     lhsT_scale=scales[i][:, cols],
                     rhs=w_codes[:, cols].bitcast(FP8X4),
@@ -205,59 +217,110 @@ def tile_parallelretention_pb_kernel(tc, x, Wq, bq, kv, decay_mask, out_0, out_1
                     stop=(c == PASSES - 1),
                 )
 
-        def e_piece(g, j0, j1):
-            r0, n, i0 = groups[g]
-            if j0 == 0:
-                ep[("t", g)] = work.tile([P, n, QD], F32, tag="t", name="t")
-                ep[("y", g)] = work.tile([P, n, QD], F32, tag="y", name="y")
+        def run_matmuls(i):
+            q = qp.tile([P, 2, QD], F32, tag="q", name="q_ps")
+            for k in range(2):
+                x_matmuls(i + k, q[:, k, :])
+                q_ps[i + k] = q[:, k : k + 1, :]
+            q_ps[(i, 2)] = q[:]
+
+        def single_matmuls(i):
+            q = tp.tile([P, 1, QD], F32, tag="tp", name="q_single")
+            x_matmuls(i, q[:, 0, :])
+            q_ps[(i, 1)] = q[:]
+
+        def e_bias(i, n):
+            g, j = tiles[i]
+            if j == 0:
+                ep[("t", g)] = work.tile([P, groups[g][1], QD], F32, tag="t", name="t")
+                ep[("y", g)] = work.tile([P, groups[g][1], QD], F32, tag="y", name="y")
                 ep[("sums", g)] = []
-            t = ep[("t", g)]
-            y = ep[("y", g)]
+            nc.vector.tensor_tensor(out=ep[("t", g)][:, j : j + n, :], in0=q_ps[(i, n)], in1=b4[:, 0:n, :], op=ALU.add)
+
+        def e_product(i, n):
+            g, j = tiles[i]
             sums = work.tile([P, 2], F32, tag="sums", name="sums", bufs=6)
-            junk = work.tile([P, j1 - j0, QD], F32, tag="junk", name="junk")
-            nc.vector.tensor_tensor(out=t[:, j0:j1, :], in0=q_ps[g][:, j0:j1, :], in1=b4[:, j0:j1, :], op=ALU.add)
             nc.vector.scalar_tensor_tensor(
-                out=y[:, j0:j1, :], in0=t[:, j0:j1, :], scalar=1.0, in1=banks[("g", i0 // 4)][:, i0 % 4 + j0 : i0 % 4 + j1, :],
-                op0=ALU.mult, op1=ALU.mult, accum_out=sums[:, 0:1],
+                out=ep[("y", g)][:, j : j + n, :], in0=ep[("t", g)][:, j : j + n, :], scalar=1.0,
+                in1=banks[("g", i // 4)][:, i % 4 : i % 4 + n, :], op0=ALU.mult, op1=ALU.mult, accum_out=sums[:, 0:1],
             )
-            nc.scalar.activation(out=junk[:], in_=y[:, j0:j1, :], func=ACT.Square, accum_out=sums[:, 1:2])
             ep[("sums", g)].append(sums)
 
+        def e_square(i, n):
+            g, j = tiles[i]
+            junk = work.tile([P, n, QD], F32, tag="junk", name="junk")
+            nc.scalar.activation(out=junk[:], in_=ep[("y", g)][:, j : j + n, :], func=ACT.Square, accum_out=ep[("sums", g)][-1][:, 1:2])
+
+        def e_square_k(i, n, k):
+            g, j = tiles[i]
+            junk = work.tile([P, n, QD], F32, tag="junk", name="junk")
+            nc.scalar.activation(out=junk[:], in_=ep[("y", g)][:, j : j + n, :], func=ACT.Square, accum_out=ep[("sums", g)][k][:, 1:2])
 
         def e_totals(g):
-            n = groups[g][1]
             tot = tp.tile([P, 2], F32, tag="tp", name="tot")
             parts = ep[("sums", g)]
             for k, sums in enumerate(parts):
-                nc.tensor.matmul(out=tot[:], lhsT=sum_mask[n][:], rhs=sums[:], start=(k == 0), stop=(k == len(parts) - 1))
+                nc.tensor.matmul(
+                    out=tot[:], lhsT=sum_mask[groups[g][1]][:], rhs=sums[:], start=(k == 0), stop=(k == len(parts) - 1)
+                )
             ep[("tot", g)] = tot
 
-        def e_moments(g):
-            mom = work.tile([P, 2], F32, tag="mom", name="mom")
-            tot = ep[("tot", g)]
-            nc.vector.tensor_scalar(out=mom[:, 0:1], in0=tot[:, 0:1], scalar1=-1.0, scalar2=None, op0=ALU.mult)
-            nc.vector.tensor_scalar(out=mom[:, 1:2], in0=tot[:, 1:2], scalar1=EPS, scalar2=None, op0=ALU.add)
-            ep[("mom", g)] = mom
+        def e_total_column(g, col):
+            tot = tp.tile([P, 1], F32, tag="tp", name="tot_col")
+            parts = ep[("sums", g)]
+            for k, sums in enumerate(parts):
+                nc.tensor.matmul(
+                    out=tot[:], lhsT=sum_mask[groups[g][1]][:], rhs=sums[:, col : col + 1], start=(k == 0), stop=(k == len(parts) - 1)
+                )
+            ep[("tot", g, col)] = tot
 
-        def e_std(g):
-            std = work.tile([P, 1], F32, tag="std", name="std")
-            mom = ep[("mom", g)]
-            nc.scalar.activation(out=std[:], in_=ep[("tot", g)][:, 0:1], func=ACT.Sqrt, bias=mom[:, 1:2], scale=mom[:, 0:1])
-            ep[("std", g)] = std
+        def mean_of(g):
+            return ep[("tot", g, 0)][:] if ("tot", g, 0) in ep else ep[("tot", g)][:, 0:1]
+
+        def square_of(g):
+            return ep[("tot", g, 1)][:] if ("tot", g, 1) in ep else ep[("tot", g)][:, 1:2]
+
+        def e_mom0(g):
+            ep[("mom0", g)] = work.tile([P, 1], F32, tag="mom0", name="mom0")
+            nc.scalar.activation(out=ep[("mom0", g)][:], in_=ep[("tot", g)][:, 0:1], func=ACT.Copy, scale=-1.0)
+
+        def e_mom1(g):
+            ep[("mom1", g)] = work.tile([P, 1], F32, tag="mom1", name="mom1")
+            nc.scalar.activation(out=ep[("mom1", g)][:], in_=ep[("tot", g)][:, 1:2], func=ACT.Copy, bias=EPS)
 
         def e_rstd(g):
-            rstd = work.tile([P, 1], F32, tag="rstd", name="rstd")
-            nc.vector.reciprocal(out=rstd[:], in_=ep[("std", g)][:])
-            ep[("rstd", g)] = rstd
+            ep[("rstd", g)] = work.tile([P, 1], F32, tag="rstd", name="rstd")
+            nc.scalar.activation(
+                out=ep[("rstd", g)][:], in_=ep[("tot", g)][:, 0:1], func=ACT.Abs_reciprocal_sqrt, bias=ep[("mom1", g)][:],
+                scale=ep[("mom0", g)][:],
+            )
 
         def e_normalise(g):
-            n = groups[g][1]
-            res = work.tile([P, n, QD], F32, tag="res", name="res")
-            nc.vector.tensor_scalar(
-                out=res[:], in0=ep[("y", g)][:], scalar1=ep[("mom", g)][:, 0:1], scalar2=ep[("rstd", g)][:],
+            ep[("res", g)] = work.tile([P, groups[g][1], QD], F32, tag="res", name="res")
+            if g in ACT_NORM:
+                nmr = work.tile([P, 1], F32, tag="nmr", name="nmr")
+                nc.scalar.activation(out=nmr[:], in_=ep[("mom0", g)][:], func=ACT.Copy, scale=ep[("rstd", g)][:])
+                nc.scalar.activation(
+                    out=ep[("res", g)][:], in_=ep[("y", g)][:], func=ACT.Identity, bias=nmr[:], scale=ep[("rstd", g)][:]
+                )
+                return
+            eng = nc.gpsimd if g in GPSIMD_NORM else nc.vector
+            eng.tensor_scalar(
+                out=ep[("res", g)][:], in0=ep[("y", g)][:], scalar1=ep[("mom0", g)][:], scalar2=ep[("rstd", g)][:],
                 op0=ALU.add, op1=ALU.mult,
             )
-            ep[("res", g)] = res
+
+        def e_centre(g):
+            ep[("d", g)] = work.tile([P, groups[g][1], QD], F32, tag="d", name="d")
+            nc.vector.tensor_scalar(
+                out=ep[("d", g)][:], in0=ep[("y", g)][:], scalar1=mean_of(g), scalar2=None, op0=ALU.subtract
+            )
+
+        def e_scale(g):
+            ep[("res", g)] = work.tile([P, groups[g][1], QD], F32, tag="res", name="res")
+            nc.vector.tensor_scalar(
+                out=ep[("res", g)][:], in0=ep[("d", g)][:], scalar1=ep[("rstd", g)][:], scalar2=None, op0=ALU.mult
+            )
 
         def e_store0(g):
             r0, n, i0 = groups[g]
@@ -266,65 +329,61 @@ def tile_parallelretention_pb_kernel(tc, x, Wq, bq, kv, decay_mask, out_0, out_1
             )
 
         def e_amax(g):
-            n = groups[g][1]
-            amax = work.tile([P, n], F32, tag="amax", name="amax")
-            nc.vector.tensor_reduce(out=amax[:], in_=ep[("res", g)][:], axis=AXIS.X, op=ALU.max, apply_absolute_value=True)
-            ep[("amax", g)] = amax
+            ep[("amax", g)] = work.tile([P, groups[g][1]], F32, tag="amax", name="amax")
+            nc.vector.tensor_reduce(
+                out=ep[("amax", g)][:], in_=ep[("res", g)][:], axis=AXIS.X, op=ALU.max, apply_absolute_value=True
+            )
 
         def e_recip(g):
-            n = groups[g][1]
-            ramax = work.tile([P, n], F32, tag="ramax", name="ramax")
-            nc.vector.reciprocal(out=ramax[:], in_=ep[("amax", g)][:])
-            ep[("ramax", g)] = ramax
+            ep[("ramax", g)] = work.tile([P, groups[g][1]], F32, tag="ramax", name="ramax")
+            nc.vector.reciprocal(out=ep[("ramax", g)][:], in_=ep[("amax", g)][:])
 
         def e_factor(g):
-            n = groups[g][1]
-            factor = work.tile([P, n], F32, tag="factor", name="factor")
-            nc.vector.tensor_scalar(out=factor[:], in0=ep[("ramax", g)][:], scalar1=448.0, scalar2=None, op0=ALU.mult)
-            ep[("factor", g)] = factor
+            ep[("factor", g)] = work.tile([P, groups[g][1]], F32, tag="factor", name="factor")
+            nc.gpsimd.tensor_scalar(
+                out=ep[("factor", g)][:], in0=ep[("ramax", g)][:], scalar1=448.0, scalar2=0.0, op0=ALU.mult, op1=ALU.add
+            )
 
-        def e_extremes(g):
-            n = groups[g][1]
-            ext = work.tile([P, 2, n], F32, tag="ext", name="ext")
-            nc.vector.tensor_reduce(out=ext[:, 0, :], in_=ep[("y", g)][:], axis=AXIS.X, op=ALU.max)
-            nc.vector.tensor_reduce(out=ext[:, 1, :], in_=ep[("y", g)][:], axis=AXIS.X, op=ALU.min)
-            ep[("ext", g)] = ext
+        def e_extreme(g, k):
+            if k == 0:
+                ep[("ext", g)] = work.tile([P, 2, groups[g][1]], F32, tag="ext", name="ext")
+            nc.vector.tensor_reduce(
+                out=ep[("ext", g)][:, k, :], in_=ep[("y", g)][:], axis=AXIS.X, op=(ALU.max if k == 0 else ALU.min)
+            )
+
+        def e_dev(g):
+            ep[("dev", g)] = work.tile([P, 2, groups[g][1]], F32, tag="dev", name="dev")
+            nc.vector.tensor_scalar(
+                out=ep[("dev", g)][:], in0=ep[("ext", g)][:], scalar1=mean_of(g), scalar2=1.0 / 448.0,
+                op0=ALU.subtract, op1=ALU.mult,
+            )
 
         def e_spread(g):
-            n = groups[g][1]
-            dev = work.tile([P, 2, n], F32, tag="dev", name="dev")
-            spread = work.tile([P, n], F32, tag="spread", name="spread")
-            rspread = work.tile([P, n], F32, tag="rspread", name="rspread")
-            nc.vector.tensor_scalar(out=dev[:], in0=ep[("ext", g)][:], scalar1=ep[("mom", g)][:, 0:1], scalar2=None, op0=ALU.add)
+            ep[("spread", g)] = work.tile([P, groups[g][1]], F32, tag="spread", name="spread")
+            dev = ep[("dev", g)]
             nc.vector.scalar_tensor_tensor(
-                out=spread[:], in0=dev[:, 1, :], scalar=-1.0, in1=dev[:, 0, :], op0=ALU.mult, op1=ALU.max
+                out=ep[("spread", g)][:], in0=dev[:, 1, :], scalar=-1.0, in1=dev[:, 0, :], op0=ALU.mult, op1=ALU.max
             )
-            nc.vector.reciprocal(out=rspread[:], in_=spread[:])
-            ep[("rspread", g)] = rspread
 
         def e_factor_from_spread(g):
-            n = groups[g][1]
-            factor = work.tile([P, n], F32, tag="factor", name="factor")
-            nc.vector.tensor_scalar(
-                out=factor[:], in0=ep[("rspread", g)][:], scalar1=ep[("std", g)][:], scalar2=448.0, op0=ALU.mult, op1=ALU.mult
-            )
-            ep[("factor", g)] = factor
+            ep[("factor", g)] = work.tile([P, groups[g][1]], F32, tag="factor", name="factor")
+            nc.vector.reciprocal(out=ep[("factor", g)][:], in_=ep[("spread", g)][:])
 
-        def e_cast(g, j):
+        def e_cast(g, j, on_scalar):
             n = groups[g][1]
-            if j == 0:
+            if ("o8", g) not in ep:
                 ep[("o8", g)] = work.tile([P, n, QD], FP8, tag="o8", name="o8")
             o8 = ep[("o8", g)]
-            res = ep[("res", g)]
+            src = ep[("d", g)] if ("d", g) in ep else ep[("res", g)]
             factor = ep[("factor", g)]
-            if j in SCALAR_CASTS:
+            if on_scalar:
                 nc.scalar.activation(
-                    out=o8[:, j, :], in_=res[:, j, :], func=ACT.Identity, bias=zero_col[:], scale=factor[:, j : j + 1],
+                    out=o8[:, j, :], in_=src[:, j, :], func=ACT.Identity, bias=zero_col[:], scale=factor[:, j : j + 1],
                     saturate=False,
                 )
             else:
                 nc.vector.tensor_scalar(
-                    out=o8[:, j, :], in0=res[:, j, :], scalar1=factor[:, j : j + 1], scalar2=None, op0=ALU.mult,
+                    out=o8[:, j, :], in0=src[:, j, :], scalar1=factor[:, j : j + 1], scalar2=None, op0=ALU.mult,
                     saturate=False,
                 )
 
@@ -334,52 +393,6 @@ def tile_parallelretention_pb_kernel(tc, x, Wq, bq, kv, decay_mask, out_0, out_1
                 out=o1_rows[r0 : r0 + P * n, :].rearrange("(p j) q -> p (j q)", j=n),
                 in_=ep[("o8", g)][:].bitcast(U8).rearrange("p j q -> p (j q)"),
             )
-
-        def tile_in(i):
-            if i == n_tiles - 1:
-                for c in range(PASSES):
-                    x_transposes_pass(i, c)
-                    x_copy_pass(i, c)
-                    x_quantize_pass(i, c)
-                return
-            for h in range(2):
-                x_transposes(i, h)
-                x_copy(i, h)
-            x_quantize(i)
-
-        def kv_in_turn(g):
-            kv_transposes(g)
-            kv_copy(g)
-
-        def finish(pending):
-            for g in pending:
-                e_totals(g)
-            for g in pending:
-                if g == len(groups) - 1:
-                    e_extremes(g)
-                e_moments(g)
-                e_std(g)
-                if g == len(groups) - 1:
-                    e_spread(g)
-                e_rstd(g)
-                e_normalise(g)
-                e_store0(g)
-                if g == len(groups) - 1:
-                    e_factor_from_spread(g)
-                else:
-                    e_amax(g)
-                    e_recip(g)
-                    e_factor(g)
-                for j in range(groups[g][1]):
-                    e_cast(g, j)
-                e_store1(g)
-
-        def bring(i):
-            if i % 4 == 0:
-                for k in range(i, i + 4):
-                    if k in first_of:
-                        kv_in_turn(first_of[k])
-            tile_in(i)
 
         first_of = dict((i0, g) for g, (r0, n, i0) in enumerate(groups))
         last_of = dict((i0 + n - 1, g) for g, (r0, n, i0) in enumerate(groups))
@@ -392,61 +405,177 @@ def tile_parallelretention_pb_kernel(tc, x, Wq, bq, kv, decay_mask, out_0, out_1
                         load_order.append(("kv", first_of[k]))
             load_order.append(("x", i))
 
-        with tc.manual_schedule(engines={mybir.EngineType.PE, mybir.EngineType.SP}):
-            for what, k in load_order:
-                if what == "x":
-                    g, j = tiles[k]
-                    r0, n, i0 = groups[g]
-                    rows = x_rows[r0 : r0 + P * n, :].rearrange("(p j) e -> p j e", j=n)
-                    if k < WHOLE_FROM:
-                        for h in range(2):
-                            nc.sync.dma_start(out=x_in[k][h][:], in_=rows[:, j, (E // 2) * h : (E // 2) * (h + 1)])
-                    else:
-                        nc.sync.dma_start(out=x_in[k][0][:], in_=rows[:, j, :])
-                elif what == "w":
-                    nc.sync.dma_start(out=w_in[k][:], in_=Wq[:, (E // 2) * k : (E // 2) * (k + 1)])
-                elif what == "kv":
-                    r0, n, i0 = groups[k]
-                    nc.sync.dma_start(out=kv_in[k][:], in_=kv_rows[r0 : r0 + P * n, :].rearrange("(p j) k -> p j k", j=n))
-                elif what == "d":
-                    nc.sync.dma_start(out=d_in[:], in_=decay_mask.rearrange("o j i -> (o j) i"))
+        def load(what, k):
+            if what == "x":
+                g, j = tiles[k]
+                r0, n, i0 = groups[g]
+                rows = x_rows[r0 : r0 + P * n, :].rearrange("(p j) e -> p j e", j=n)
+                if k < WHOLE_FROM:
+                    for h in range(2):
+                        nc.sync.dma_start(out=x_in[k][h][:], in_=rows[:, j, (E // 2) * h : (E // 2) * (h + 1)])
                 else:
-                    nc.sync.dma_start(out=brow[0:1, :], in_=bq.rearrange("(o q) -> o q", o=1))
+                    nc.sync.dma_start(out=x_in[k][0][:], in_=rows[:, j, :])
+            elif what == "w":
+                nc.sync.dma_start(out=w_in[k][:], in_=Wq[:, (E // 2) * k : (E // 2) * (k + 1)])
+            elif what == "kv":
+                r0, n, i0 = groups[k]
+                nc.sync.dma_start(out=kv_in[k][:], in_=kv_rows[r0 : r0 + P * n, :].rearrange("(p j) k -> p j k", j=n))
+            elif what == "d":
+                nc.sync.dma_start(out=d_in[:], in_=decay_mask.rearrange("o j i -> (o j) i"))
+            else:
+                nc.sync.dma_start(out=brow[0:1, :], in_=bq.rearrange("(o q) -> o q", o=1))
 
-            tile_in(0)
-            tile_in(1)
+        with tc.manual_schedule():
+            for what, k in load_order:
+                load(what, k)
+
+            for i in range(2):
+                for h in range(2):
+                    x_transposes(i, h)
+                    x_copy(i, h)
+                x_quantize(i)
             for h in range(2):
                 transpose_half(("w", h), w_in[h][:].bitcast(F32))
-                copy_half(("w", h), w_grouped, h, True)
-            w_quantize()
-            kv_in_turn(0)
+                copy_half(("w", h), w_grouped, h)
+            kv_transposes(0)
             d_transpose()
-            d_copy()
             bias_matmul()
-            for j in range(4):
+            kv_copy(0)
+            d_copy()
+            for j in range(2):
                 bias_copy(j)
-            bring(2)
-            g_matmul(0)
-            g_matmul(1)
-            bring(3)
+            w_quantize()
 
-            waiting = []
-            for first in range(0, n_tiles, RUN):
-                run = range(first, first + RUN)
-                last_run = first + RUN == n_tiles
-                for i in run:
-                    g, j = tiles[i]
-                    x_matmuls(i)
-                    if last_run:
-                        e_piece(g, j, j + 1)
-                if not last_run and first + 1 in last_of:
-                    g, j = tiles[first + 1]
-                    e_piece(g, 0, j + 1)
-                finish(waiting)
-                waiting = [last_of[i] for i in run if i in last_of]
-                if first + 2 * RUN < n_tiles:
-                    bring(first + 2 * RUN)
-                    for i in range(first + RUN, first + (3 if first + 3 * RUN == n_tiles else 2) * RUN):
-                        g_matmul(i)
-                    bring(first + 2 * RUN + 1)
-            finish(waiting)
+            for i in (4, 5):
+                if i in SORTED:
+                    x_sort(i, 0)
+                    x_sort(i, 1)
+            for i in (2, 3):
+                for h in range(2):
+                    x_transposes(i, h)
+                    x_copy(i, h)
+                if i == 2:
+                    x_quantize(i)
+            for i in range(4):
+                g_matmul(i)
+            run_matmuls(0)
+
+            fin = None
+            for r in range(2, N_RUNS):
+                a, b, e = 2 * r, 2 * r + 1, 2 * (r - 2)
+                last = r == N_RUNS - 1
+                if a % 4 == 0:
+                    for k in range(a, a + 4):
+                        if k in first_of:
+                            kv_transposes(first_of[k])
+                if fin is not None:
+                    e_mom0(fin)
+                    e_mom1(fin)
+                    e_rstd(fin)
+                x_transposes(a, 0)
+                x_copy(a, 0)
+                x_transposes(a, 1)
+                x_copy(a, 1)
+                e_bias(e, 2)
+                if a % 4 == 0:
+                    for k in range(a, a + 4):
+                        if k in first_of:
+                            kv_copy(first_of[k])
+                x_quantize(b - 2)
+                for i in (a + 2, b + 2):
+                    if i in SORTED:
+                        x_sort(i, 0)
+                        x_sort(i, 1)
+                if fin is not None:
+                    e_normalise(fin)
+                    e_store0(fin)
+                e_product(e, 2)
+                g_matmul(a)
+                g_matmul(b)
+                if last:
+                    for c in range(PASSES):
+                        x_transposes_pass(b, c)
+                    for c in range(3):
+                        x_copy_pass(b, c)
+                    e_square(e, 2)
+                    x_copy_pass(b, 3)
+                else:
+                    e_square(e, 2)
+                    for h in range(2):
+                        x_transposes(b, h)
+                        x_copy(b, h)
+                if fin is not None:
+                    e_amax(fin)
+                x_quantize(a)
+                if fin is not None:
+                    e_recip(fin)
+                    e_factor(fin)
+                run_matmuls(a - 2)
+                if fin is not None and not last:
+                    for j in range(groups[fin][1]):
+                        e_cast(fin, j, True)
+                    e_store1(fin)
+                if e + 1 in last_of:
+                    e_totals(last_of[e + 1])
+                    nxt_fin = last_of[e + 1]
+                else:
+                    nxt_fin = None
+                if not last:
+                    fin = nxt_fin
+
+            for c in range(3):
+                x_quantize_pass(15, c)
+            e_bias(12, 2)
+            x_quantize_pass(15, 3)
+            single_matmuls(14)
+            single_matmuls(15)
+            for j in range(groups[fin][1]):
+                e_cast(fin, j, True)
+            e_store1(fin)
+            e_mom0(3)
+            e_mom1(3)
+            e_rstd(3)
+            e_product(12, 2)
+            e_bias(14, 1)
+            e_normalise(3)
+            e_store0(3)
+            e_bias(15, 1)
+            e_product(14, 1)
+            e_product(15, 1)
+            e_square_k(12, 2, 0)
+            e_square_k(14, 1, 0)
+            e_square_k(15, 1, 1)
+            e_totals(4)
+            e_total_column(5, 0)
+            e_totals(5)
+            e_amax(3)
+            e_extreme(5, 0)
+            e_extreme(5, 1)
+            e_recip(3)
+            e_factor(3)
+            e_mom0(4)
+            e_mom1(4)
+            e_rstd(4)
+            e_mom0(5)
+            e_mom1(5)
+            e_rstd(5)
+            e_dev(5)
+            e_centre(5)
+            e_normalise(4)
+            e_store0(4)
+            e_spread(5)
+            e_amax(4)
+            e_factor_from_spread(5)
+            e_scale(5)
+            e_store0(5)
+            for j in range(2):
+                e_cast(3, j, True)
+            e_store1(3)
+            e_recip(4)
+            e_cast(5, 0, False)
+            e_cast(5, 1, True)
+            e_store1(5)
+            e_factor(4)
+            e_cast(4, 0, True)
+            e_cast(4, 1, False)
+            e_store1(4)

@@ -156,6 +156,10 @@ def tile_parallelretention_pb_kernel(tc, x, Wq, bq, kv, decay_mask, out_0, out_1
             g, j = tiles[i]
             nc.tensor.matmul(out=banks[("g", i // 4)][:, i % 4, :], lhsT=kvT[g][:, j, :], rhs=dT[:], start=True, stop=True)
 
+        def g_again(i):
+            g, j = tiles[i]
+            nc.tensor.matmul(out=banks[("g", i // 4)][:, i % 4, :], lhsT=kvT[g][:, j, :], rhs=dT[:], start=True, stop=True)
+
         def w_quantize():
             nc.vector.quantize_mx(out=w_codes[:].bitcast(FP8X4), scales=w_scales[:], in_=w_grouped[:])
 
@@ -330,8 +334,9 @@ def tile_parallelretention_pb_kernel(tc, x, Wq, bq, kv, decay_mask, out_0, out_1
 
         def e_amax(g):
             ep[("amax", g)] = work.tile([P, groups[g][1]], F32, tag="amax", name="amax")
+            src = ep[("d", g)] if ("d", g) in ep else ep[("res", g)]
             nc.vector.tensor_reduce(
-                out=ep[("amax", g)][:], in_=ep[("res", g)][:], axis=AXIS.X, op=ALU.max, apply_absolute_value=True
+                out=ep[("amax", g)][:], in_=src[:], axis=AXIS.X, op=ALU.max, apply_absolute_value=True
             )
 
         def e_recip(g):
@@ -342,6 +347,12 @@ def tile_parallelretention_pb_kernel(tc, x, Wq, bq, kv, decay_mask, out_0, out_1
             ep[("factor", g)] = work.tile([P, groups[g][1]], F32, tag="factor", name="factor")
             nc.gpsimd.tensor_scalar(
                 out=ep[("factor", g)][:], in0=ep[("ramax", g)][:], scalar1=448.0, scalar2=0.0, op0=ALU.mult, op1=ALU.add
+            )
+
+        def e_factor_v(g):
+            ep[("factor", g)] = work.tile([P, groups[g][1]], F32, tag="factor", name="factor")
+            nc.vector.tensor_scalar(
+                out=ep[("factor", g)][:], in0=ep[("ramax", g)][:], scalar1=448.0, scalar2=None, op0=ALU.mult
             )
 
         def e_extreme(g, k):
@@ -458,16 +469,14 @@ def tile_parallelretention_pb_kernel(tc, x, Wq, bq, kv, decay_mask, out_0, out_1
                     x_quantize(i)
             for i in range(4):
                 g_matmul(i)
+            kv_transposes(1)
+            kv_copy(1)
             run_matmuls(0)
 
             fin = None
             for r in range(2, N_RUNS):
                 a, b, e = 2 * r, 2 * r + 1, 2 * (r - 2)
                 last = r == N_RUNS - 1
-                if a % 4 == 0:
-                    for k in range(a, a + 4):
-                        if k in first_of:
-                            kv_transposes(first_of[k])
                 if fin is not None:
                     e_mom0(fin)
                     e_mom1(fin)
@@ -477,21 +486,19 @@ def tile_parallelretention_pb_kernel(tc, x, Wq, bq, kv, decay_mask, out_0, out_1
                 x_transposes(a, 1)
                 x_copy(a, 1)
                 e_bias(e, 2)
-                if a % 4 == 0:
-                    for k in range(a, a + 4):
-                        if k in first_of:
-                            kv_copy(first_of[k])
                 x_quantize(b - 2)
-                for i in (a + 2, b + 2):
-                    if i in SORTED:
-                        x_sort(i, 0)
-                        x_sort(i, 1)
+                if b in SORTED:
+                    x_sort(b, 0)
+                    x_sort(b, 1)
                 if fin is not None:
                     e_normalise(fin)
                     e_store0(fin)
                 e_product(e, 2)
                 g_matmul(a)
                 g_matmul(b)
+                kvs = [first_of[k] for k in range(a + 2, a + 6) if k in first_of and k < n_tiles] if a % 4 == 2 else []
+                for k in kvs:
+                    kv_transposes(k)
                 if last:
                     for c in range(PASSES):
                         x_transposes_pass(b, c)
@@ -507,6 +514,11 @@ def tile_parallelretention_pb_kernel(tc, x, Wq, bq, kv, decay_mask, out_0, out_1
                 if fin is not None:
                     e_amax(fin)
                 x_quantize(a)
+                for k in kvs:
+                    kv_copy(k)
+                if a + 2 in SORTED:
+                    x_sort(a + 2, 0)
+                    x_sort(a + 2, 1)
                 if fin is not None:
                     e_recip(fin)
                     e_factor(fin)
@@ -537,11 +549,11 @@ def tile_parallelretention_pb_kernel(tc, x, Wq, bq, kv, decay_mask, out_0, out_1
             e_rstd(3)
             e_product(12, 2)
             e_bias(14, 1)
-            e_normalise(3)
-            e_store0(3)
             e_bias(15, 1)
             e_product(14, 1)
             e_product(15, 1)
+            e_normalise(3)
+            e_store0(3)
             e_square_k(12, 2, 0)
             e_square_k(14, 1, 0)
             e_square_k(15, 1, 1)
@@ -549,33 +561,31 @@ def tile_parallelretention_pb_kernel(tc, x, Wq, bq, kv, decay_mask, out_0, out_1
             e_total_column(5, 0)
             e_totals(5)
             e_amax(3)
-            e_extreme(5, 0)
-            e_extreme(5, 1)
+            e_centre(5)
             e_recip(3)
-            e_factor(3)
             e_mom0(4)
             e_mom1(4)
             e_rstd(4)
+            e_factor(3)
             e_mom0(5)
             e_mom1(5)
             e_rstd(5)
-            e_dev(5)
-            e_centre(5)
             e_normalise(4)
             e_store0(4)
-            e_spread(5)
+            e_amax(5)
             e_amax(4)
-            e_factor_from_spread(5)
+            e_recip(5)
             e_scale(5)
             e_store0(5)
+            e_factor_v(5)
+            e_recip(4)
+            e_factor_v(4)
             for j in range(2):
                 e_cast(3, j, True)
             e_store1(3)
-            e_recip(4)
             e_cast(5, 0, False)
             e_cast(5, 1, True)
             e_store1(5)
-            e_factor(4)
             e_cast(4, 0, True)
             e_cast(4, 1, False)
             e_store1(4)

@@ -469,14 +469,16 @@ def tile_parallelretention_pb_kernel(tc, x, Wq, bq, kv, decay_mask, out_0, out_1
                     x_quantize(i)
             for i in range(4):
                 g_matmul(i)
-            kv_transposes(1)
-            kv_copy(1)
             run_matmuls(0)
 
             fin = None
             for r in range(2, N_RUNS):
                 a, b, e = 2 * r, 2 * r + 1, 2 * (r - 2)
                 last = r == N_RUNS - 1
+                if a % 4 == 0:
+                    for k in range(a, a + 4):
+                        if k in first_of:
+                            kv_transposes(first_of[k])
                 if fin is not None:
                     e_mom0(fin)
                     e_mom1(fin)
@@ -486,6 +488,10 @@ def tile_parallelretention_pb_kernel(tc, x, Wq, bq, kv, decay_mask, out_0, out_1
                 x_transposes(a, 1)
                 x_copy(a, 1)
                 e_bias(e, 2)
+                if a % 4 == 0:
+                    for k in range(a, a + 4):
+                        if k in first_of:
+                            kv_copy(first_of[k])
                 x_quantize(b - 2)
                 if b in SORTED:
                     x_sort(b, 0)
@@ -496,9 +502,6 @@ def tile_parallelretention_pb_kernel(tc, x, Wq, bq, kv, decay_mask, out_0, out_1
                 e_product(e, 2)
                 g_matmul(a)
                 g_matmul(b)
-                kvs = [first_of[k] for k in range(a + 2, a + 6) if k in first_of and k < n_tiles] if a % 4 == 2 else []
-                for k in kvs:
-                    kv_transposes(k)
                 if last:
                     for c in range(PASSES):
                         x_transposes_pass(b, c)
@@ -514,8 +517,6 @@ def tile_parallelretention_pb_kernel(tc, x, Wq, bq, kv, decay_mask, out_0, out_1
                 if fin is not None:
                     e_amax(fin)
                 x_quantize(a)
-                for k in kvs:
-                    kv_copy(k)
                 if a + 2 in SORTED:
                     x_sort(a + 2, 0)
                     x_sort(a + 2, 1)

@@ -25,6 +25,7 @@ N_RUNS = B // 2
 WHOLE_FROM = 4
 SORTED = ()
 ACT_NORM = ()
+KV_RUNS = (2, 3, 5)
 GPSIMD_NORM = ()
 ACT_CASTS = (1, 3)
 
@@ -50,7 +51,8 @@ def tile_parallelretention_pb_kernel(tc, x, Wq, bq, kv, decay_mask, out_0, out_1
         xin = ctx.enter_context(tc.tile_pool(name="xin", bufs=1))
         work = ctx.enter_context(tc.tile_pool(name="work", bufs=3))
         tp = ctx.enter_context(tc.psum_pool(name="tp", bufs=5))
-        gp = ctx.enter_context(tc.psum_pool(name="gp", bufs=2))
+        mp = ctx.enter_context(tc.psum_pool(name="mp", bufs=1))
+        gp = ctx.enter_context(tc.psum_pool(name="gp", bufs=1))
         qp = ctx.enter_context(tc.psum_pool(name="qp", bufs=1))
 
         ident_b = const.tile([P, P], BF16, name="ident_b")
@@ -77,7 +79,7 @@ def tile_parallelretention_pb_kernel(tc, x, Wq, bq, kv, decay_mask, out_0, out_1
                 sum_mask[n] = mean_mask
 
         d_in = xin.tile([P, L], BF16, name="d_in")
-        kv_in = [xin.tile([P, n, L], BF16, name="kv_in%d" % g) for g, (r0, n, i0) in enumerate(groups)]
+        kv_in = [xin.tile([P, 4, L], BF16, name="kv_in%d" % q) for q in range(n_tiles // 4)]
         w_in = [xin.tile([P, E // 2], BF16, name="w_in%d" % h) for h in range(2)]
         x_in = [
             [xin.tile([P, E // 2], BF16, name="x_in%d_%d" % (i, h)) for h in range(2)]
@@ -91,7 +93,7 @@ def tile_parallelretention_pb_kernel(tc, x, Wq, bq, kv, decay_mask, out_0, out_1
                 return x_in[i][h][:].bitcast(F32)
             return x_in[i][0][:, (E // 2) * h : (E // 2) * (h + 1)].bitcast(F32)
 
-        kvT = [const.tile([P, n, P], BF16, name="kvT%d" % g) for g, (r0, n, i0) in enumerate(groups)]
+        kvT = [const.tile([P, 4, P], BF16, name="kvT%d" % q) for q in range(n_tiles // 4)]
         dT = const.tile([P, QD], BF16, name="dT")
         b4 = const.tile([P, 2, QD], F32, name="b4")
         w_grouped = const.tile([P, E], BF16, name="w_grouped", align_bytes=64)
@@ -120,19 +122,22 @@ def tile_parallelretention_pb_kernel(tc, x, Wq, bq, kv, decay_mask, out_0, out_1
                     nc.tensor.transpose(bank[:, c, u, :], words[:, c, u, :], ident_f[:])
             banks[key] = bank
 
-        def copy_half(key, dst_tile, h):
+        def copy_half(key, dst_tile, h, on_vector=False):
             dst = dst_tile[:].bitcast(F32)[:, 512 * h : 512 * (h + 1)].rearrange("p (c r u) -> p c r u", c=2, u=2)
-            nc.scalar.copy(out=dst, in_=banks[key][:].rearrange("p c u r -> p c r u"))
+            src = banks[key][:].rearrange("p c u r -> p c r u")
+            if on_vector:
+                nc.vector.tensor_copy(out=dst, in_=src)
+            else:
+                nc.scalar.copy(out=dst, in_=src)
 
-        def kv_transposes(g):
-            n = groups[g][1]
-            bank = tp.tile([P, n, P], BF16, tag="tp", name="kvT_ps")
-            for j in range(n):
-                nc.tensor.transpose(bank[:, j, :], kv_in[g][:, j, :], ident_b[:])
-            banks[("kv", g)] = bank
+        def kv_transposes(q):
+            bank = mp.tile([P, 4, P], BF16, tag="mp", name="kvT_ps")
+            for j in range(4):
+                nc.tensor.transpose(bank[:, j, :], kv_in[q][:, j, :], ident_b[:])
+            banks[("kv", q)] = bank
 
-        def kv_copy(g):
-            nc.vector.tensor_copy(out=kvT[g][:], in_=banks[("kv", g)][:])
+        def kv_copy(q):
+            nc.vector.tensor_copy(out=kvT[q][:], in_=banks[("kv", q)][:])
 
         def d_transpose():
             bank = tp.tile([P, QD], BF16, tag="tp", name="dT_ps")
@@ -150,15 +155,11 @@ def tile_parallelretention_pb_kernel(tc, x, Wq, bq, kv, decay_mask, out_0, out_1
         def bias_copy(j):
             nc.vector.tensor_copy(out=b4[:, j, :], in_=banks["b"][:])
 
-        def g_matmul(i):
-            if i % 4 == 0:
-                banks[("g", i // 4)] = gp.tile([P, 4, QD], F32, tag="g", name="g_ps")
-            g, j = tiles[i]
-            nc.tensor.matmul(out=banks[("g", i // 4)][:, i % 4, :], lhsT=kvT[g][:, j, :], rhs=dT[:], start=True, stop=True)
-
-        def g_again(i):
-            g, j = tiles[i]
-            nc.tensor.matmul(out=banks[("g", i // 4)][:, i % 4, :], lhsT=kvT[g][:, j, :], rhs=dT[:], start=True, stop=True)
+        def g_matmuls(i, n, pool):
+            bank = pool.tile([P, n, QD], F32, tag="tp" if pool is tp else "g", name="g_ps")
+            for k in range(i, i + n):
+                nc.tensor.matmul(out=bank[:, k - i, :], lhsT=kvT[k // 4][:, k % 4, :], rhs=dT[:], start=True, stop=True)
+                banks[("g", k)] = (bank, k - i)
 
         def w_quantize():
             nc.vector.quantize_mx(out=w_codes[:].bitcast(FP8X4), scales=w_scales[:], in_=w_grouped[:])
@@ -246,7 +247,7 @@ def tile_parallelretention_pb_kernel(tc, x, Wq, bq, kv, decay_mask, out_0, out_1
             sums = work.tile([P, 2], F32, tag="sums", name="sums", bufs=6)
             nc.vector.scalar_tensor_tensor(
                 out=ep[("y", g)][:, j : j + n, :], in0=ep[("t", g)][:, j : j + n, :], scalar=1.0,
-                in1=banks[("g", i // 4)][:, i % 4 : i % 4 + n, :], op0=ALU.mult, op1=ALU.mult, accum_out=sums[:, 0:1],
+                in1=banks[("g", i)][0][:, banks[("g", i)][1] : banks[("g", i)][1] + n, :], op0=ALU.mult, op1=ALU.mult, accum_out=sums[:, 0:1],
             )
             ep[("sums", g)].append(sums)
 
@@ -260,8 +261,8 @@ def tile_parallelretention_pb_kernel(tc, x, Wq, bq, kv, decay_mask, out_0, out_1
             junk = work.tile([P, n, QD], F32, tag="junk", name="junk")
             nc.scalar.activation(out=junk[:], in_=ep[("y", g)][:, j : j + n, :], func=ACT.Square, accum_out=ep[("sums", g)][k][:, 1:2])
 
-        def e_totals(g):
-            tot = tp.tile([P, 2], F32, tag="tp", name="tot")
+        def e_totals(g, pool):
+            tot = pool.tile([P, 2], F32, tag="tp" if pool is tp else "mp", name="tot")
             parts = ep[("sums", g)]
             for k, sums in enumerate(parts):
                 nc.tensor.matmul(
@@ -430,7 +431,7 @@ def tile_parallelretention_pb_kernel(tc, x, Wq, bq, kv, decay_mask, out_0, out_1
                 nc.sync.dma_start(out=w_in[k][:], in_=Wq[:, (E // 2) * k : (E // 2) * (k + 1)])
             elif what == "kv":
                 r0, n, i0 = groups[k]
-                nc.sync.dma_start(out=kv_in[k][:], in_=kv_rows[r0 : r0 + P * n, :].rearrange("(p j) k -> p j k", j=n))
+                nc.sync.dma_start(out=kv_in[i0 // 4][:, i0 % 4 : i0 % 4 + n, :], in_=kv_rows[r0 : r0 + P * n, :].rearrange("(p j) k -> p j k", j=n))
             elif what == "d":
                 nc.sync.dma_start(out=d_in[:], in_=decay_mask.rearrange("o j i -> (o j) i"))
             else:
@@ -444,148 +445,142 @@ def tile_parallelretention_pb_kernel(tc, x, Wq, bq, kv, decay_mask, out_0, out_1
                 for h in range(2):
                     x_transposes(i, h)
                     x_copy(i, h)
-                x_quantize(i)
+                if i == 0:
+                    x_quantize(i)
             for h in range(2):
                 transpose_half(("w", h), w_in[h][:].bitcast(F32))
-                copy_half(("w", h), w_grouped, h)
+                copy_half(("w", h), w_grouped, h, h == 0)
+            x_quantize(1)
             kv_transposes(0)
-            d_transpose()
-            bias_matmul()
             kv_copy(0)
+            d_transpose()
             d_copy()
+            bias_matmul()
             for j in range(2):
                 bias_copy(j)
             w_quantize()
-
-            for i in (4, 5):
-                if i in SORTED:
-                    x_sort(i, 0)
-                    x_sort(i, 1)
             for i in (2, 3):
                 for h in range(2):
                     x_transposes(i, h)
                     x_copy(i, h)
                 if i == 2:
                     x_quantize(i)
-            for i in range(4):
-                g_matmul(i)
             run_matmuls(0)
 
-            fin = None
+            fin_norm = None
+            fin_cast = None
             for r in range(2, N_RUNS):
                 a, b, e = 2 * r, 2 * r + 1, 2 * (r - 2)
                 last = r == N_RUNS - 1
-                if a % 4 == 0:
-                    for k in range(a, a + 4):
-                        if k in first_of:
-                            kv_transposes(first_of[k])
-                if fin is not None:
-                    e_mom0(fin)
-                    e_mom1(fin)
-                    e_rstd(fin)
                 x_transposes(a, 0)
-                x_copy(a, 0)
+                if fin_norm is not None:
+                    e_totals(fin_norm, mp)
+                g_matmuls(e, 2, gp)
                 x_transposes(a, 1)
+                x_copy(a, 0)
+                if fin_norm is not None:
+                    e_mom0(fin_norm)
+                    e_mom1(fin_norm)
                 x_copy(a, 1)
+                if fin_norm is not None:
+                    e_rstd(fin_norm)
                 e_bias(e, 2)
-                if a % 4 == 0:
-                    for k in range(a, a + 4):
-                        if k in first_of:
-                            kv_copy(first_of[k])
                 x_quantize(b - 2)
-                if b in SORTED:
-                    x_sort(b, 0)
-                    x_sort(b, 1)
-                if fin is not None:
-                    e_normalise(fin)
-                    e_store0(fin)
+                if fin_cast is not None:
+                    e_amax(fin_cast)
                 e_product(e, 2)
-                g_matmul(a)
-                g_matmul(b)
+                if r in KV_RUNS:
+                    kv_transposes(KV_RUNS.index(r) + 1)
+                    kv_copy(KV_RUNS.index(r) + 1)
+                if fin_cast is not None:
+                    e_recip(fin_cast)
+                    e_factor(fin_cast)
                 if last:
                     for c in range(PASSES):
                         x_transposes_pass(b, c)
-                    for c in range(3):
+                    for c in range(4):
                         x_copy_pass(b, c)
                     e_square(e, 2)
-                    x_copy_pass(b, 3)
+                    for c in range(4, PASSES):
+                        x_copy_pass(b, c)
                 else:
+                    x_transposes(b, 0)
+                    x_transposes(b, 1)
                     e_square(e, 2)
-                    for h in range(2):
-                        x_transposes(b, h)
-                        x_copy(b, h)
-                if fin is not None:
-                    e_amax(fin)
-                x_quantize(a)
-                if a + 2 in SORTED:
-                    x_sort(a + 2, 0)
-                    x_sort(a + 2, 1)
-                if fin is not None:
-                    e_recip(fin)
-                    e_factor(fin)
-                run_matmuls(a - 2)
-                if fin is not None and not last:
-                    for j in range(groups[fin][1]):
-                        e_cast(fin, j, True)
-                    e_store1(fin)
-                if e + 1 in last_of:
-                    e_totals(last_of[e + 1])
-                    nxt_fin = last_of[e + 1]
-                else:
-                    nxt_fin = None
-                if not last:
-                    fin = nxt_fin
+                    x_copy(b, 0)
+                    x_copy(b, 1)
 
-            for c in range(3):
+                x_quantize(a)
+                if fin_norm is not None:
+                    e_normalise(fin_norm)
+                    e_store0(fin_norm)
+                if fin_cast is not None and not last:
+                    for j in range(groups[fin_cast][1]):
+                        e_cast(fin_cast, j, True)
+                    e_store1(fin_cast)
+                if not last:
+                    run_matmuls(a - 2)
+                    fin_cast = fin_norm
+                    fin_norm = last_of.get(e + 1)
+
+            g_matmuls(12, 4, tp)
+            run_matmuls(12)
+            for c in range(PASSES):
                 x_quantize_pass(15, c)
+            for j in range(groups[fin_cast][1]):
+                e_cast(fin_cast, j, True)
+            e_store1(fin_cast)
             e_bias(12, 2)
-            x_quantize_pass(15, 3)
             single_matmuls(14)
             single_matmuls(15)
-            for j in range(groups[fin][1]):
-                e_cast(fin, j, True)
-            e_store1(fin)
+            e_totals(3, tp)
+            e_bias(14, 1)
+            e_product(12, 2)
             e_mom0(3)
             e_mom1(3)
             e_rstd(3)
-            e_product(12, 2)
-            e_bias(14, 1)
+            e_amax(2)
             e_bias(15, 1)
             e_product(14, 1)
+            e_recip(2)
             e_product(15, 1)
             e_normalise(3)
             e_store0(3)
+            e_factor_v(2)
             e_square_k(12, 2, 0)
             e_square_k(14, 1, 0)
             e_square_k(15, 1, 1)
-            e_totals(4)
+            e_totals(4, tp)
             e_total_column(5, 0)
-            e_totals(5)
+            e_totals(5, tp)
             e_amax(3)
-            e_centre(5)
-            e_recip(3)
             e_mom0(4)
             e_mom1(4)
+            e_cast(2, 0, True)
             e_rstd(4)
-            e_factor(3)
+            e_cast(2, 1, True)
+            e_store1(2)
             e_mom0(5)
             e_mom1(5)
+            e_centre(5)
+            e_recip(3)
             e_rstd(5)
             e_normalise(4)
             e_store0(4)
+            e_factor_v(3)
             e_amax(5)
+            e_cast(3, 0, True)
+            e_cast(3, 1, True)
+            e_store1(3)
             e_amax(4)
             e_recip(5)
             e_scale(5)
             e_store0(5)
-            e_factor_v(5)
             e_recip(4)
+            e_factor_v(5)
             e_factor_v(4)
-            for j in range(2):
-                e_cast(3, j, True)
-            e_store1(3)
-            e_cast(5, 0, False)
-            e_cast(5, 1, True)
+            e_cast(5, 0, True)
+            e_cast(5, 1, False)
             e_store1(5)
             e_cast(4, 0, True)
             e_cast(4, 1, False)

@@ -237,8 +237,8 @@ def tile_parallelretention_pb_kernel(tc, x, Wq, bq, kv, decay_mask, out_0, out_1
         def e_bias(i, n):
             g, j = tiles[i]
             if j == 0:
-                ep[("t", g)] = work.tile([P, groups[g][1], QD], F32, tag="t", name="t")
-                ep[("y", g)] = work.tile([P, groups[g][1], QD], F32, tag="y", name="y")
+                ep[("t", g)] = work.tile([P, groups[g][1], QD], F32, tag="t", name="t", bufs=6)
+                ep[("y", g)] = work.tile([P, groups[g][1], QD], F32, tag="y", name="y", bufs=6)
                 ep[("sums", g)] = []
             nc.vector.tensor_tensor(out=ep[("t", g)][:, j : j + n, :], in0=q_ps[(i, n)], in1=b4[:, 0:n, :], op=ALU.add)
 
@@ -301,7 +301,7 @@ def tile_parallelretention_pb_kernel(tc, x, Wq, bq, kv, decay_mask, out_0, out_1
             )
 
         def e_normalise(g):
-            ep[("res", g)] = work.tile([P, groups[g][1], QD], F32, tag="res", name="res")
+            ep[("res", g)] = work.tile([P, groups[g][1], QD], F32, tag="res", name="res", bufs=6)
             if g in ACT_NORM:
                 nmr = work.tile([P, 1], F32, tag="nmr", name="nmr")
                 nc.scalar.activation(out=nmr[:], in_=ep[("mom0", g)][:], func=ACT.Copy, scale=ep[("rstd", g)][:])
@@ -316,16 +316,20 @@ def tile_parallelretention_pb_kernel(tc, x, Wq, bq, kv, decay_mask, out_0, out_1
             )
 
         def e_centre(g):
-            ep[("d", g)] = work.tile([P, groups[g][1], QD], F32, tag="d", name="d")
+            ep[("d", g)] = work.tile([P, groups[g][1], QD], F32, tag="d", name="d", bufs=6)
             nc.vector.tensor_scalar(
                 out=ep[("d", g)][:], in0=ep[("y", g)][:], scalar1=mean_of(g), scalar2=None, op0=ALU.subtract
             )
 
         def e_scale(g):
-            ep[("res", g)] = work.tile([P, groups[g][1], QD], F32, tag="res", name="res")
+            ep[("res", g)] = work.tile([P, groups[g][1], QD], F32, tag="res", name="res", bufs=6)
             nc.vector.tensor_scalar(
                 out=ep[("res", g)][:], in0=ep[("d", g)][:], scalar1=ep[("rstd", g)][:], scalar2=None, op0=ALU.mult
             )
+
+        def e_wide(g):
+            ep[("wide", g)] = work.tile([P, groups[g][1], QD], F32, tag="wide", name="wide", bufs=6)
+            nc.scalar.activation(out=ep[("wide", g)][:], in_=ep[("d", g)][:], func=ACT.Copy, scale=448.0)
 
         def e_store0(g):
             r0, n, i0 = groups[g]
@@ -384,10 +388,10 @@ def tile_parallelretention_pb_kernel(tc, x, Wq, bq, kv, decay_mask, out_0, out_1
         def e_cast(g, j, on_scalar):
             n = groups[g][1]
             if ("o8", g) not in ep:
-                ep[("o8", g)] = work.tile([P, n, QD], FP8, tag="o8", name="o8")
+                ep[("o8", g)] = work.tile([P, n, QD], FP8, tag="o8", name="o8", bufs=6)
             o8 = ep[("o8", g)]
-            src = ep[("d", g)] if ("d", g) in ep else ep[("res", g)]
-            factor = ep[("factor", g)]
+            src = ep[("wide", g)] if ("wide", g) in ep else (ep[("d", g)] if ("d", g) in ep else ep[("res", g)])
+            factor = ep[("ramax", g)] if ("wide", g) in ep else ep[("factor", g)]
             if on_scalar:
                 nc.scalar.activation(
                     out=o8[:, j, :], in_=src[:, j, :], func=ACT.Identity, bias=zero_col[:], scale=factor[:, j : j + 1],
@@ -472,11 +476,13 @@ def tile_parallelretention_pb_kernel(tc, x, Wq, bq, kv, decay_mask, out_0, out_1
             for r in range(2, N_RUNS):
                 a, b, e = 2 * r, 2 * r + 1, 2 * (r - 2)
                 last = r == N_RUNS - 1
+                if a % 4 == 0:
+                    kv_transposes(a // 4)
                 x_transposes(a, 0)
                 if fin_norm is not None:
-                    e_totals(fin_norm, mp)
-                g_matmuls(e, 2, gp)
+                    e_totals(fin_norm, mp if last else tp)
                 x_transposes(a, 1)
+                g_matmuls(e, 2, gp)
                 x_copy(a, 0)
                 if fin_norm is not None:
                     e_mom0(fin_norm)
@@ -485,13 +491,12 @@ def tile_parallelretention_pb_kernel(tc, x, Wq, bq, kv, decay_mask, out_0, out_1
                 if fin_norm is not None:
                     e_rstd(fin_norm)
                 e_bias(e, 2)
+                if a % 4 == 0:
+                    kv_copy(a // 4)
                 x_quantize(b - 2)
                 if fin_cast is not None:
                     e_amax(fin_cast)
                 e_product(e, 2)
-                if r in KV_RUNS:
-                    kv_transposes(KV_RUNS.index(r) + 1)
-                    kv_copy(KV_RUNS.index(r) + 1)
                 if fin_cast is not None:
                     e_recip(fin_cast)
                     e_factor(fin_cast)
@@ -546,13 +551,15 @@ def tile_parallelretention_pb_kernel(tc, x, Wq, bq, kv, decay_mask, out_0, out_1
             e_product(15, 1)
             e_normalise(3)
             e_store0(3)
-            e_factor_v(2)
             e_square_k(12, 2, 0)
             e_square_k(14, 1, 0)
             e_square_k(15, 1, 1)
+            e_total_column(4, 0)
             e_totals(4, tp)
             e_total_column(5, 0)
             e_totals(5, tp)
+            e_centre(4)
+            e_factor_v(2)
             e_amax(3)
             e_mom0(4)
             e_mom1(4)
@@ -560,28 +567,28 @@ def tile_parallelretention_pb_kernel(tc, x, Wq, bq, kv, decay_mask, out_0, out_1
             e_rstd(4)
             e_cast(2, 1, True)
             e_store1(2)
+            e_centre(5)
+            e_amax(4)
             e_mom0(5)
             e_mom1(5)
-            e_centre(5)
-            e_recip(3)
+            e_wide(4)
             e_rstd(5)
-            e_normalise(4)
-            e_store0(4)
-            e_factor_v(3)
+            e_wide(5)
+            e_recip(3)
             e_amax(5)
-            e_cast(3, 0, True)
-            e_cast(3, 1, True)
-            e_store1(3)
-            e_amax(4)
+            e_scale(4)
+            e_store0(4)
+            e_recip(4)
+            e_factor_v(3)
             e_recip(5)
             e_scale(5)
             e_store0(5)
-            e_recip(4)
-            e_factor_v(5)
-            e_factor_v(4)
+            e_cast(4, 0, True)
+            e_cast(3, 0, False)
+            e_cast(3, 1, False)
+            e_store1(3)
+            e_cast(4, 1, True)
+            e_store1(4)
             e_cast(5, 0, True)
             e_cast(5, 1, False)
             e_store1(5)
-            e_cast(4, 0, True)
-            e_cast(4, 1, False)
-            e_store1(4)

@@ -23,7 +23,7 @@ GROUPS = (4, 4, 2, 2, 2, 2)
 LAST = len(GROUPS) - 1
 N_RUNS = B // 2
 WHOLE_FROM = 4
-SORTED = ()
+SORTED = (6, 8, 10, 12)
 ACT_NORM = ()
 KV_RUNS = (2, 3, 5)
 GPSIMD_NORM = ()
@@ -497,6 +497,12 @@ def tile_parallelretention_pb_kernel(tc, x, Wq, bq, kv, decay_mask, out_0, out_1
                 if fin_cast is not None:
                     e_amax(fin_cast)
                 e_product(e, 2)
+                if a + 2 in SORTED:
+                    x_sort(a + 2, 0)
+                    x_sort(a + 2, 1)
+                if b + 2 in SORTED:
+                    x_sort(b + 2, 0)
+                    x_sort(b + 2, 1)
                 if fin_cast is not None:
                     e_recip(fin_cast)
                     e_factor(fin_cast)

@@ -20,14 +20,9 @@ PASSES = E // (4 * P)
 FLOPS = 2 * B * L * E * QD + 2 * B * L * L * QD
 
 GROUPS = (4, 4, 2, 2, 2, 2)
-LAST = len(GROUPS) - 1
 N_RUNS = B // 2
-WHOLE_FROM = 4
-SORTED = (6, 8, 10, 12)
-ACT_NORM = ()
-KV_RUNS = (2, 3, 5)
-GPSIMD_NORM = ()
-ACT_CASTS = (1, 3)
+IN_HALVES = 4
+SORTED = (6, 8, 10, 12, 14)
 
 
 def tile_parallelretention_pb_kernel(tc, x, Wq, bq, kv, decay_mask, out_0, out_1):
@@ -45,13 +40,14 @@ def tile_parallelretention_pb_kernel(tc, x, Wq, bq, kv, decay_mask, out_0, out_1
             tiles.append((len(groups) - 1, j))
     n_tiles = len(tiles)
     assert n_tiles == B
+    last_of = dict((i0 + n - 1, g) for g, (r0, n, i0) in enumerate(groups))
 
     with ExitStack() as ctx:
         const = ctx.enter_context(tc.tile_pool(name="const", bufs=1))
         xin = ctx.enter_context(tc.tile_pool(name="xin", bufs=1))
         work = ctx.enter_context(tc.tile_pool(name="work", bufs=3))
-        tp = ctx.enter_context(tc.psum_pool(name="tp", bufs=5))
-        mp = ctx.enter_context(tc.psum_pool(name="mp", bufs=1))
+        tp = ctx.enter_context(tc.psum_pool(name="tp", bufs=1))
+        mp = ctx.enter_context(tc.psum_pool(name="mp", bufs=2))
         gp = ctx.enter_context(tc.psum_pool(name="gp", bufs=1))
         qp = ctx.enter_context(tc.psum_pool(name="qp", bufs=1))
 
@@ -69,33 +65,33 @@ def tile_parallelretention_pb_kernel(tc, x, Wq, bq, kv, decay_mask, out_0, out_1
         nc.scalar.activation(out=warm[:], in_=one_col[:], func=ACT.Abs_reciprocal_sqrt)
         make_identity(nc, ident_f[:])
         make_identity(nc, ident_b[:])
-        sum_mask = {}
+        mean_mask = {}
         for n in GROUPS:
-            if n not in sum_mask:
+            if n not in mean_mask:
                 blockdiag = const.tile([P, P], F32, name="blockdiag%d" % n)
                 make_block_diagonal(nc, blockdiag[:], P // n)
-                mean_mask = const.tile([P, P], F32, name="mean_mask%d" % n)
-                nc.vector.tensor_scalar(out=mean_mask[:], in0=blockdiag[:], scalar1=1.0 / (L * QD), scalar2=None, op0=ALU.mult)
-                sum_mask[n] = mean_mask
+                mask = const.tile([P, P], F32, name="mean_mask%d" % n)
+                nc.vector.tensor_scalar(out=mask[:], in0=blockdiag[:], scalar1=1.0 / (L * QD), scalar2=None, op0=ALU.mult)
+                mean_mask[n] = mask
 
         d_in = xin.tile([P, L], BF16, name="d_in")
         kv_in = [xin.tile([P, 4, L], BF16, name="kv_in%d" % q) for q in range(n_tiles // 4)]
         w_in = [xin.tile([P, E // 2], BF16, name="w_in%d" % h) for h in range(2)]
         x_in = [
             [xin.tile([P, E // 2], BF16, name="x_in%d_%d" % (i, h)) for h in range(2)]
-            if i < WHOLE_FROM
+            if i < IN_HALVES
             else [xin.tile([P, E], BF16, name="x_in%d" % i)]
             for i in range(n_tiles)
         ]
 
         def x_words(i, h):
-            if i < WHOLE_FROM:
+            if i < IN_HALVES:
                 return x_in[i][h][:].bitcast(F32)
             return x_in[i][0][:, (E // 2) * h : (E // 2) * (h + 1)].bitcast(F32)
 
         kvT = [const.tile([P, 4, P], BF16, name="kvT%d" % q) for q in range(n_tiles // 4)]
         dT = const.tile([P, QD], BF16, name="dT")
-        b4 = const.tile([P, 2, QD], F32, name="b4")
+        bias = const.tile([P, 2, QD], F32, name="bias")
         w_grouped = const.tile([P, E], BF16, name="w_grouped", align_bytes=64)
         w_codes = const.tile([P, E // 4], U32, name="w_codes", align_bytes=64)
         w_scales = const.tile([P, E // 4], U8, name="w_scales", align_bytes=64)
@@ -104,116 +100,108 @@ def tile_parallelretention_pb_kernel(tc, x, Wq, bq, kv, decay_mask, out_0, out_1
         grouped = {}
         codes = {}
         scales = {}
-        q_ps = {}
-        ep = {}
         sorted_words = {}
+        q_ps = {}
+        g_ps = {}
+        ep = {}
 
-        def transpose_half(key, words):
-            bank = tp.tile([P, 2, 2, P], F32, tag="tp", name="xT")
+        def transposes(turn, h, words, in_order):
+            tag = "turned%d" % (2 * (turn % 2) + (h + turn // 2) % 2)
+            bank = tp.tile([P, 2, 2, P], F32, tag=tag, name="turned")
             for c in range(2):
                 for u in range(2):
-                    nc.tensor.transpose(bank[:, c, u, :], words[:, 256 * c + u : 256 * (c + 1) : 2], ident_f[:])
-            banks[key] = bank
+                    src = words[:, c, u, :] if in_order else words[:, 2 * P * c + u : 2 * P * (c + 1) : 2]
+                    nc.tensor.transpose(bank[:, c, u, :], src, ident_f[:])
+            banks[(turn, h)] = bank
 
-        def transpose_sorted_half(key, words):
-            bank = tp.tile([P, 2, 2, P], F32, tag="tp", name="xT")
-            for c in range(2):
-                for u in range(2):
-                    nc.tensor.transpose(bank[:, c, u, :], words[:, c, u, :], ident_f[:])
-            banks[key] = bank
+        def turn_of(i):
+            return i if i < 2 else i + 1
 
-        def copy_half(key, dst_tile, h, on_vector=False):
-            dst = dst_tile[:].bitcast(F32)[:, 512 * h : 512 * (h + 1)].rearrange("p (c r u) -> p c r u", c=2, u=2)
-            src = banks[key][:].rearrange("p c u r -> p c r u")
+        def copy_out(turn, h, dst_tile, on_vector=False):
+            dst = dst_tile[:].bitcast(F32)[:, 4 * P * h : 4 * P * (h + 1)].rearrange("p (c r u) -> p c r u", c=2, u=2)
+            src = banks[(turn, h)][:].rearrange("p c u r -> p c r u")
             if on_vector:
                 nc.vector.tensor_copy(out=dst, in_=src)
             else:
                 nc.scalar.copy(out=dst, in_=src)
 
-        def kv_transposes(q):
-            bank = mp.tile([P, 4, P], BF16, tag="mp", name="kvT_ps")
-            for j in range(4):
-                nc.tensor.transpose(bank[:, j, :], kv_in[q][:, j, :], ident_b[:])
-            banks[("kv", q)] = bank
-
-        def kv_copy(q):
-            nc.vector.tensor_copy(out=kvT[q][:], in_=banks[("kv", q)][:])
-
-        def d_transpose():
-            bank = tp.tile([P, QD], BF16, tag="tp", name="dT_ps")
-            nc.tensor.transpose(bank[:], d_in[:], ident_b[:])
-            banks["d"] = bank
-
-        def d_copy():
-            nc.vector.tensor_copy(out=dT[:], in_=banks["d"][:])
-
-        def bias_matmul():
-            bank = tp.tile([P, QD], F32, tag="tp", name="b_ps")
-            nc.tensor.matmul(out=bank[:], lhsT=ones_b[:], rhs=brow[:], start=True, stop=True)
-            banks["b"] = bank
-
-        def bias_copy(j):
-            nc.vector.tensor_copy(out=b4[:, j, :], in_=banks["b"][:])
-
-        def g_matmuls(i, n, pool):
-            bank = pool.tile([P, n, QD], F32, tag="tp" if pool is tp else "g", name="g_ps")
-            for k in range(i, i + n):
-                nc.tensor.matmul(out=bank[:, k - i, :], lhsT=kvT[k // 4][:, k % 4, :], rhs=dT[:], start=True, stop=True)
-                banks[("g", k)] = (bank, k - i)
-
         def w_quantize():
             nc.vector.quantize_mx(out=w_codes[:].bitcast(FP8X4), scales=w_scales[:], in_=w_grouped[:])
 
-        def x_sort(i, h):
-            if h == 0:
-                sorted_words[i] = work.tile([P, 2, 2, 2, P], F32, tag="sorted", name="sorted", bufs=2)
-            nc.vector.tensor_copy(
-                out=sorted_words[i][:, h, :, :, :], in_=x_words(i, h).rearrange("p (c r u) -> p c u r", c=2, u=2)
-            )
+        def x_sort(i):
+            sorted_words[i] = work.tile([P, 2, 2, 2, P], F32, tag="sorted", name="sorted", bufs=2)
+            for h in range(2):
+                nc.vector.tensor_copy(
+                    out=sorted_words[i][:, h, :, :, :], in_=x_words(i, h).rearrange("p (c r u) -> p c u r", c=2, u=2)
+                )
 
         def x_transposes(i, h):
             if i in SORTED:
-                transpose_sorted_half(("x", i, h), sorted_words[i][:, h, :, :, :])
+                transposes(turn_of(i), h, sorted_words[i][:, h, :, :, :], True)
             else:
-                transpose_half(("x", i, h), x_words(i, h))
+                transposes(turn_of(i), h, x_words(i, h), False)
+
+        def x_tiles(i):
+            grouped[i] = work.tile([P, E], BF16, tag="grouped", name="grouped", bufs=4, align_bytes=64)
+            codes[i] = const.tile([P, E // 4], U32, name="codes%d" % i, align_bytes=64)
+            scales[i] = const.tile([P, E // 4], U8, name="scales%d" % i, align_bytes=64)
 
         def x_copy(i, h):
             if h == 0:
-                grouped[i] = work.tile([P, E], BF16, tag="grouped", name="grouped", bufs=4, align_bytes=64)
-            copy_half(("x", i, h), grouped[i], h)
+                x_tiles(i)
+            copy_out(turn_of(i), h, grouped[i])
 
         def x_quantize(i):
-            codes[i] = const.tile([P, E // 4], U32, name="codes%d" % i, align_bytes=64)
-            scales[i] = const.tile([P, E // 4], U8, name="scales%d" % i, align_bytes=64)
             nc.vector.quantize_mx(out=codes[i][:].bitcast(FP8X4), scales=scales[i][:], in_=grouped[i][:])
-
-        def x_transposes_pass(i, c):
-            words = x_words(i, c // 2)
-            bank = tp.tile([P, 2, P], F32, tag="tp", name="xT_pass")
-            for u in range(2):
-                nc.tensor.transpose(bank[:, u, :], words[:, 256 * (c % 2) + u : 256 * (c % 2 + 1) : 2], ident_f[:])
-            banks[("xp", i, c)] = bank
 
         def x_copy_pass(i, c):
             if c == 0:
-                grouped[i] = work.tile([P, E], BF16, tag="grouped", name="grouped", bufs=4, align_bytes=64)
-            dst = grouped[i][:].bitcast(F32)[:, 256 * c : 256 * (c + 1)].rearrange("p (r u) -> p r u", u=2)
-            nc.scalar.copy(out=dst, in_=banks[("xp", i, c)][:].rearrange("p u r -> p r u"))
+                x_tiles(i)
+            dst = grouped[i][:].bitcast(F32)[:, 2 * P * c : 2 * P * (c + 1)].rearrange("p (r u) -> p r u", u=2)
+            nc.scalar.copy(out=dst, in_=banks[(turn_of(i), c // 2)][:, c % 2, :, :].rearrange("p u r -> p r u"))
 
         def x_quantize_pass(i, c):
-            if c == 0:
-                codes[i] = const.tile([P, E // 4], U32, name="codes%d" % i, align_bytes=64)
-                scales[i] = const.tile([P, E // 4], U8, name="scales%d" % i, align_bytes=64)
             cols = slice(c * P, (c + 1) * P)
             nc.vector.quantize_mx(
                 out=codes[i][:, cols].bitcast(FP8X4), scales=scales[i][:, cols], in_=grouped[i][:, 4 * P * c : 4 * P * (c + 1)]
             )
 
-        def x_matmuls(i, q):
+        def kv_transposes(q):
+            banks[("kv", q)] = mp.tile([P, 4, P], BF16, tag="mp", name="kvT_ps")
+            for j in range(4):
+                nc.tensor.transpose(banks[("kv", q)][:, j, :], kv_in[q][:, j, :], ident_b[:])
+
+        def kv_copy(q):
+            nc.vector.tensor_copy(out=kvT[q][:], in_=banks[("kv", q)][:])
+
+        def d_transpose():
+            banks["d"] = mp.tile([P, QD], BF16, tag="mp", name="dT_ps")
+            nc.tensor.transpose(banks["d"][:], d_in[:], ident_b[:])
+
+        def d_copy():
+            nc.vector.tensor_copy(out=dT[:], in_=banks["d"][:])
+
+        def bias_matmul():
+            banks["b"] = gp.tile([P, QD], F32, tag="g", name="b_ps")
+            nc.tensor.matmul(out=banks["b"][:], lhsT=ones_b[:], rhs=brow[:], start=True, stop=True)
+
+        def bias_copies():
+            for j in range(2):
+                nc.vector.tensor_copy(out=bias[:, j, :], in_=banks["b"][:])
+
+        def g_matmuls(i, n):
+            bank = gp.tile([P, n, QD], F32, tag="g", name="g_ps")
+            for k in range(n):
+                nc.tensor.matmul(
+                    out=bank[:, k, :], lhsT=kvT[(i + k) // 4][:, (i + k) % 4, :], rhs=dT[:], start=True, stop=True
+                )
+                g_ps[i + k] = (bank, k)
+
+        def x_matmuls(i, out):
             for c in range(PASSES):
                 cols = slice(c * P, (c + 1) * P)
                 nc.tensor.matmul_mx(
-                    out=q,
+                    out=out,
                     lhsT=codes[i][:, cols].bitcast(FP8X4),
                     lhsT_scale=scales[i][:, cols],
                     rhs=w_codes[:, cols].bitcast(FP8X4),
@@ -222,15 +210,14 @@ def tile_parallelretention_pb_kernel(tc, x, Wq, bq, kv, decay_mask, out_0, out_1
                     stop=(c == PASSES - 1),
                 )
 
-        def run_matmuls(i):
+        def pair_matmuls(i):
             q = qp.tile([P, 2, QD], F32, tag="q", name="q_ps")
-            for k in range(2):
+            for k in (1, 0):
                 x_matmuls(i + k, q[:, k, :])
-                q_ps[i + k] = q[:, k : k + 1, :]
             q_ps[(i, 2)] = q[:]
 
         def single_matmuls(i):
-            q = tp.tile([P, 1, QD], F32, tag="tp", name="q_single")
+            q = mp.tile([P, 1, QD], F32, tag="mp", name="q_single")
             x_matmuls(i, q[:, 0, :])
             q_ps[(i, 1)] = q[:]
 
@@ -240,85 +227,60 @@ def tile_parallelretention_pb_kernel(tc, x, Wq, bq, kv, decay_mask, out_0, out_1
                 ep[("t", g)] = work.tile([P, groups[g][1], QD], F32, tag="t", name="t", bufs=6)
                 ep[("y", g)] = work.tile([P, groups[g][1], QD], F32, tag="y", name="y", bufs=6)
                 ep[("sums", g)] = []
-            nc.vector.tensor_tensor(out=ep[("t", g)][:, j : j + n, :], in0=q_ps[(i, n)], in1=b4[:, 0:n, :], op=ALU.add)
+            nc.vector.tensor_tensor(out=ep[("t", g)][:, j : j + n, :], in0=q_ps[(i, n)], in1=bias[:, 0:n, :], op=ALU.add)
 
         def e_product(i, n):
             g, j = tiles[i]
+            bank, k = g_ps[i]
             sums = work.tile([P, 2], F32, tag="sums", name="sums", bufs=6)
             nc.vector.scalar_tensor_tensor(
                 out=ep[("y", g)][:, j : j + n, :], in0=ep[("t", g)][:, j : j + n, :], scalar=1.0,
-                in1=banks[("g", i)][0][:, banks[("g", i)][1] : banks[("g", i)][1] + n, :], op0=ALU.mult, op1=ALU.mult, accum_out=sums[:, 0:1],
+                in1=bank[:, k : k + n, :], op0=ALU.mult, op1=ALU.mult, accum_out=sums[:, 0:1],
             )
+            ep[("part", i)] = sums
             ep[("sums", g)].append(sums)
 
         def e_square(i, n):
             g, j = tiles[i]
             junk = work.tile([P, n, QD], F32, tag="junk", name="junk")
-            nc.scalar.activation(out=junk[:], in_=ep[("y", g)][:, j : j + n, :], func=ACT.Square, accum_out=ep[("sums", g)][-1][:, 1:2])
+            nc.scalar.activation(
+                out=junk[:], in_=ep[("y", g)][:, j : j + n, :], func=ACT.Square, accum_out=ep[("part", i)][:, 1:2]
+            )
 
-        def e_square_k(i, n, k):
-            g, j = tiles[i]
-            junk = work.tile([P, n, QD], F32, tag="junk", name="junk")
-            nc.scalar.activation(out=junk[:], in_=ep[("y", g)][:, j : j + n, :], func=ACT.Square, accum_out=ep[("sums", g)][k][:, 1:2])
-
-        def e_totals(g, pool):
-            tot = pool.tile([P, 2], F32, tag="tp" if pool is tp else "mp", name="tot")
+        def e_totals(g, first, n_cols, pool, tag, key):
+            tot = pool.tile([P, n_cols], F32, tag=tag, name="tot")
             parts = ep[("sums", g)]
             for k, sums in enumerate(parts):
                 nc.tensor.matmul(
-                    out=tot[:], lhsT=sum_mask[groups[g][1]][:], rhs=sums[:], start=(k == 0), stop=(k == len(parts) - 1)
+                    out=tot[:], lhsT=mean_mask[groups[g][1]][:], rhs=sums[:, first : first + n_cols], start=(k == 0),
+                    stop=(k == len(parts) - 1),
                 )
-            ep[("tot", g)] = tot
+            ep[(key, g)] = tot
 
-        def e_total_column(g, col):
-            tot = tp.tile([P, 1], F32, tag="tp", name="tot_col")
-            parts = ep[("sums", g)]
-            for k, sums in enumerate(parts):
-                nc.tensor.matmul(
-                    out=tot[:], lhsT=sum_mask[groups[g][1]][:], rhs=sums[:, col : col + 1], start=(k == 0), stop=(k == len(parts) - 1)
-                )
-            ep[("tot", g, col)] = tot
-
-        def mean_of(g):
-            return ep[("tot", g, 0)][:] if ("tot", g, 0) in ep else ep[("tot", g)][:, 0:1]
-
-        def square_of(g):
-            return ep[("tot", g, 1)][:] if ("tot", g, 1) in ep else ep[("tot", g)][:, 1:2]
-
-        def e_mom0(g):
-            ep[("mom0", g)] = work.tile([P, 1], F32, tag="mom0", name="mom0")
-            nc.scalar.activation(out=ep[("mom0", g)][:], in_=ep[("tot", g)][:, 0:1], func=ACT.Copy, scale=-1.0)
-
-        def e_mom1(g):
-            ep[("mom1", g)] = work.tile([P, 1], F32, tag="mom1", name="mom1")
-            nc.scalar.activation(out=ep[("mom1", g)][:], in_=ep[("tot", g)][:, 1:2], func=ACT.Copy, bias=EPS)
+        def e_moments(g):
+            ep[("neg_mean", g)] = work.tile([P, 1], F32, tag="neg_mean", name="neg_mean")
+            ep[("square", g)] = work.tile([P, 1], F32, tag="square", name="square")
+            nc.scalar.activation(out=ep[("neg_mean", g)][:], in_=ep[("tot", g)][:, 0:1], func=ACT.Copy, scale=-1.0)
+            nc.scalar.activation(out=ep[("square", g)][:], in_=ep[("tot", g)][:, 1:2], func=ACT.Copy, bias=EPS)
 
         def e_rstd(g):
             ep[("rstd", g)] = work.tile([P, 1], F32, tag="rstd", name="rstd")
             nc.scalar.activation(
-                out=ep[("rstd", g)][:], in_=ep[("tot", g)][:, 0:1], func=ACT.Abs_reciprocal_sqrt, bias=ep[("mom1", g)][:],
-                scale=ep[("mom0", g)][:],
+                out=ep[("rstd", g)][:], in_=ep[("tot", g)][:, 0:1], func=ACT.Abs_reciprocal_sqrt, bias=ep[("square", g)][:],
+                scale=ep[("neg_mean", g)][:],
             )
 
         def e_normalise(g):
             ep[("res", g)] = work.tile([P, groups[g][1], QD], F32, tag="res", name="res", bufs=6)
-            if g in ACT_NORM:
-                nmr = work.tile([P, 1], F32, tag="nmr", name="nmr")
-                nc.scalar.activation(out=nmr[:], in_=ep[("mom0", g)][:], func=ACT.Copy, scale=ep[("rstd", g)][:])
-                nc.scalar.activation(
-                    out=ep[("res", g)][:], in_=ep[("y", g)][:], func=ACT.Identity, bias=nmr[:], scale=ep[("rstd", g)][:]
-                )
-                return
-            eng = nc.gpsimd if g in GPSIMD_NORM else nc.vector
-            eng.tensor_scalar(
-                out=ep[("res", g)][:], in0=ep[("y", g)][:], scalar1=ep[("mom0", g)][:], scalar2=ep[("rstd", g)][:],
+            nc.vector.tensor_scalar(
+                out=ep[("res", g)][:], in0=ep[("y", g)][:], scalar1=ep[("neg_mean", g)][:], scalar2=ep[("rstd", g)][:],
                 op0=ALU.add, op1=ALU.mult,
             )
 
         def e_centre(g):
-            ep[("d", g)] = work.tile([P, groups[g][1], QD], F32, tag="d", name="d", bufs=6)
+            ep[("d", g)] = work.tile([P, groups[g][1], QD], F32, tag="d", name="d")
             nc.vector.tensor_scalar(
-                out=ep[("d", g)][:], in0=ep[("y", g)][:], scalar1=mean_of(g), scalar2=None, op0=ALU.subtract
+                out=ep[("d", g)][:], in0=ep[("y", g)][:], scalar1=ep[("mean", g)][:], scalar2=None, op0=ALU.subtract
             )
 
         def e_scale(g):
@@ -328,79 +290,41 @@ def tile_parallelretention_pb_kernel(tc, x, Wq, bq, kv, decay_mask, out_0, out_1
             )
 
         def e_wide(g):
-            ep[("wide", g)] = work.tile([P, groups[g][1], QD], F32, tag="wide", name="wide", bufs=6)
+            ep[("wide", g)] = work.tile([P, groups[g][1], QD], F32, tag="wide", name="wide")
             nc.scalar.activation(out=ep[("wide", g)][:], in_=ep[("d", g)][:], func=ACT.Copy, scale=448.0)
 
         def e_store0(g):
             r0, n, i0 = groups[g]
-            nc.sync.dma_start(
-                out=o0_rows[r0 : r0 + P * n, :].rearrange("(p j) q -> p j q", j=n), in_=ep[("res", g)][:]
-            )
+            nc.sync.dma_start(out=o0_rows[r0 : r0 + P * n, :].rearrange("(p j) q -> p j q", j=n), in_=ep[("res", g)][:])
 
         def e_amax(g):
             ep[("amax", g)] = work.tile([P, groups[g][1]], F32, tag="amax", name="amax")
             src = ep[("d", g)] if ("d", g) in ep else ep[("res", g)]
-            nc.vector.tensor_reduce(
-                out=ep[("amax", g)][:], in_=src[:], axis=AXIS.X, op=ALU.max, apply_absolute_value=True
-            )
+            nc.vector.tensor_reduce(out=ep[("amax", g)][:], in_=src[:], axis=AXIS.X, op=ALU.max, apply_absolute_value=True)
 
         def e_recip(g):
             ep[("ramax", g)] = work.tile([P, groups[g][1]], F32, tag="ramax", name="ramax")
             nc.vector.reciprocal(out=ep[("ramax", g)][:], in_=ep[("amax", g)][:])
 
-        def e_factor(g):
+        def e_factor(g, eng):
             ep[("factor", g)] = work.tile([P, groups[g][1]], F32, tag="factor", name="factor")
-            nc.gpsimd.tensor_scalar(
+            eng.tensor_scalar(
                 out=ep[("factor", g)][:], in0=ep[("ramax", g)][:], scalar1=448.0, scalar2=0.0, op0=ALU.mult, op1=ALU.add
             )
 
-        def e_factor_v(g):
-            ep[("factor", g)] = work.tile([P, groups[g][1]], F32, tag="factor", name="factor")
-            nc.vector.tensor_scalar(
-                out=ep[("factor", g)][:], in0=ep[("ramax", g)][:], scalar1=448.0, scalar2=None, op0=ALU.mult
-            )
-
-        def e_extreme(g, k):
-            if k == 0:
-                ep[("ext", g)] = work.tile([P, 2, groups[g][1]], F32, tag="ext", name="ext")
-            nc.vector.tensor_reduce(
-                out=ep[("ext", g)][:, k, :], in_=ep[("y", g)][:], axis=AXIS.X, op=(ALU.max if k == 0 else ALU.min)
-            )
-
-        def e_dev(g):
-            ep[("dev", g)] = work.tile([P, 2, groups[g][1]], F32, tag="dev", name="dev")
-            nc.vector.tensor_scalar(
-                out=ep[("dev", g)][:], in0=ep[("ext", g)][:], scalar1=mean_of(g), scalar2=1.0 / 448.0,
-                op0=ALU.subtract, op1=ALU.mult,
-            )
-
-        def e_spread(g):
-            ep[("spread", g)] = work.tile([P, groups[g][1]], F32, tag="spread", name="spread")
-            dev = ep[("dev", g)]
-            nc.vector.scalar_tensor_tensor(
-                out=ep[("spread", g)][:], in0=dev[:, 1, :], scalar=-1.0, in1=dev[:, 0, :], op0=ALU.mult, op1=ALU.max
-            )
-
-        def e_factor_from_spread(g):
-            ep[("factor", g)] = work.tile([P, groups[g][1]], F32, tag="factor", name="factor")
-            nc.vector.reciprocal(out=ep[("factor", g)][:], in_=ep[("spread", g)][:])
-
         def e_cast(g, j, on_scalar):
-            n = groups[g][1]
             if ("o8", g) not in ep:
-                ep[("o8", g)] = work.tile([P, n, QD], FP8, tag="o8", name="o8", bufs=6)
-            o8 = ep[("o8", g)]
-            src = ep[("wide", g)] if ("wide", g) in ep else (ep[("d", g)] if ("d", g) in ep else ep[("res", g)])
+                ep[("o8", g)] = work.tile([P, groups[g][1], QD], FP8, tag="o8", name="o8", bufs=6)
+            dst = ep[("o8", g)][:, j, :]
+            src = ep[("wide", g)] if ("wide", g) in ep else ep[("res", g)]
             factor = ep[("ramax", g)] if ("wide", g) in ep else ep[("factor", g)]
             if on_scalar:
                 nc.scalar.activation(
-                    out=o8[:, j, :], in_=src[:, j, :], func=ACT.Identity, bias=zero_col[:], scale=factor[:, j : j + 1],
-                    saturate=False,
+                    out=dst, in_=src[:, j, :], func=ACT.Identity, bias=zero_col[:], scale=factor[:, j : j + 1], saturate=False
                 )
             else:
                 nc.vector.tensor_scalar(
-                    out=o8[:, j, :], in0=src[:, j, :], scalar1=factor[:, j : j + 1], scalar2=None, op0=ALU.mult,
-                    saturate=False,
+                    out=dst, in0=src[:, j, :], scalar1=factor[:, j : j + 1], scalar2=None, op0=ALU.mult, saturate=False
                 )
 
         def e_store1(g):
@@ -410,40 +334,35 @@ def tile_parallelretention_pb_kernel(tc, x, Wq, bq, kv, decay_mask, out_0, out_1
                 in_=ep[("o8", g)][:].bitcast(U8).rearrange("p j q -> p (j q)"),
             )
 
-        first_of = dict((i0, g) for g, (r0, n, i0) in enumerate(groups))
-        last_of = dict((i0 + n - 1, g) for g, (r0, n, i0) in enumerate(groups))
-
-        load_order = [("x", 0), ("x", 1), ("w", 0), ("w", 1), ("kv", 0), ("d", 0), ("b", 0)]
-        for i in range(2, n_tiles):
-            if i % 4 == 0:
-                for k in range(i, i + 4):
-                    if k in first_of:
-                        load_order.append(("kv", first_of[k]))
-            load_order.append(("x", i))
-
-        def load(what, k):
-            if what == "x":
-                g, j = tiles[k]
-                r0, n, i0 = groups[g]
-                rows = x_rows[r0 : r0 + P * n, :].rearrange("(p j) e -> p j e", j=n)
-                if k < WHOLE_FROM:
-                    for h in range(2):
-                        nc.sync.dma_start(out=x_in[k][h][:], in_=rows[:, j, (E // 2) * h : (E // 2) * (h + 1)])
-                else:
-                    nc.sync.dma_start(out=x_in[k][0][:], in_=rows[:, j, :])
-            elif what == "w":
-                nc.sync.dma_start(out=w_in[k][:], in_=Wq[:, (E // 2) * k : (E // 2) * (k + 1)])
-            elif what == "kv":
-                r0, n, i0 = groups[k]
-                nc.sync.dma_start(out=kv_in[i0 // 4][:, i0 % 4 : i0 % 4 + n, :], in_=kv_rows[r0 : r0 + P * n, :].rearrange("(p j) k -> p j k", j=n))
-            elif what == "d":
-                nc.sync.dma_start(out=d_in[:], in_=decay_mask.rearrange("o j i -> (o j) i"))
+        def load_x(i):
+            g, j = tiles[i]
+            r0, n, i0 = groups[g]
+            rows = x_rows[r0 : r0 + P * n, :].rearrange("(p j) e -> p j e", j=n)
+            if i < IN_HALVES:
+                for h in range(2):
+                    nc.sync.dma_start(out=x_in[i][h][:], in_=rows[:, j, (E // 2) * h : (E // 2) * (h + 1)])
             else:
-                nc.sync.dma_start(out=brow[0:1, :], in_=bq.rearrange("(o q) -> o q", o=1))
+                nc.sync.dma_start(out=x_in[i][0][:], in_=rows[:, j, :])
+
+        def load_kv(q):
+            n = groups[tiles[4 * q][0]][1]
+            nc.sync.dma_start(
+                out=kv_in[q][:].rearrange("p (s j) k -> p s (j k)", j=n),
+                in_=kv_rows[4 * P * q : 4 * P * (q + 1), :].rearrange("(s p j) k -> p s (j k)", p=P, j=n),
+            )
 
         with tc.manual_schedule():
-            for what, k in load_order:
-                load(what, k)
+            load_x(0)
+            load_x(1)
+            for h in range(2):
+                nc.sync.dma_start(out=w_in[h][:], in_=Wq[:, (E // 2) * h : (E // 2) * (h + 1)])
+            load_kv(0)
+            nc.sync.dma_start(out=d_in[:], in_=decay_mask.rearrange("o j i -> (o j) i"))
+            nc.sync.dma_start(out=brow[0:1, :], in_=bq.rearrange("(o q) -> o q", o=1))
+            for i in range(2, n_tiles):
+                if i > 2 and i % 4 == 0:
+                    load_kv(i // 4)
+                load_x(i)
 
             for i in range(2):
                 for h in range(2):
@@ -452,16 +371,15 @@ def tile_parallelretention_pb_kernel(tc, x, Wq, bq, kv, decay_mask, out_0, out_1
                 if i == 0:
                     x_quantize(i)
             for h in range(2):
-                transpose_half(("w", h), w_in[h][:].bitcast(F32))
-                copy_half(("w", h), w_grouped, h, h == 0)
+                transposes(2, h, w_in[h][:].bitcast(F32), False)
+                copy_out(2, h, w_grouped, h == 0)
             x_quantize(1)
             kv_transposes(0)
             kv_copy(0)
             d_transpose()
             d_copy()
             bias_matmul()
-            for j in range(2):
-                bias_copy(j)
+            bias_copies()
             w_quantize()
             for i in (2, 3):
                 for h in range(2):
@@ -469,86 +387,76 @@ def tile_parallelretention_pb_kernel(tc, x, Wq, bq, kv, decay_mask, out_0, out_1
                     x_copy(i, h)
                 if i == 2:
                     x_quantize(i)
-            run_matmuls(0)
+            pair_matmuls(0)
 
-            fin_norm = None
-            fin_cast = None
+            to_finish = None
+            to_cast = None
             for r in range(2, N_RUNS):
                 a, b, e = 2 * r, 2 * r + 1, 2 * (r - 2)
                 last = r == N_RUNS - 1
                 if a % 4 == 0:
                     kv_transposes(a // 4)
                 x_transposes(a, 0)
-                if fin_norm is not None:
-                    e_totals(fin_norm, mp if last else tp)
+                if to_finish is not None:
+                    e_totals(to_finish, 0, 2, mp, "mp", "tot")
                 x_transposes(a, 1)
-                g_matmuls(e, 2, gp)
+                g_matmuls(e, 2)
                 x_copy(a, 0)
-                if fin_norm is not None:
-                    e_mom0(fin_norm)
-                    e_mom1(fin_norm)
+                if to_finish is not None:
+                    e_moments(to_finish)
                 x_copy(a, 1)
-                if fin_norm is not None:
-                    e_rstd(fin_norm)
+                if to_finish is not None:
+                    e_rstd(to_finish)
                 e_bias(e, 2)
                 if a % 4 == 0:
                     kv_copy(a // 4)
                 x_quantize(b - 2)
-                if fin_cast is not None:
-                    e_amax(fin_cast)
+                if to_cast is not None:
+                    e_amax(to_cast)
                 e_product(e, 2)
-                if a + 2 in SORTED:
-                    x_sort(a + 2, 0)
-                    x_sort(a + 2, 1)
-                if b + 2 in SORTED:
-                    x_sort(b + 2, 0)
-                    x_sort(b + 2, 1)
-                if fin_cast is not None:
-                    e_recip(fin_cast)
-                    e_factor(fin_cast)
+                for i in (a + 2, b + 2):
+                    if i in SORTED:
+                        x_sort(i)
+                if to_cast is not None:
+                    e_recip(to_cast)
+                    e_factor(to_cast, nc.gpsimd)
+                x_transposes(b, 0)
+                x_transposes(b, 1)
                 if last:
                     for c in range(PASSES):
-                        x_transposes_pass(b, c)
-                    for c in range(4):
                         x_copy_pass(b, c)
                     e_square(e, 2)
-                    for c in range(4, PASSES):
-                        x_copy_pass(b, c)
                 else:
-                    x_transposes(b, 0)
-                    x_transposes(b, 1)
                     e_square(e, 2)
-                    x_copy(b, 0)
-                    x_copy(b, 1)
-
+                    for h in range(2):
+                        x_copy(b, h)
                 x_quantize(a)
-                if fin_norm is not None:
-                    e_normalise(fin_norm)
-                    e_store0(fin_norm)
-                if fin_cast is not None and not last:
-                    for j in range(groups[fin_cast][1]):
-                        e_cast(fin_cast, j, True)
-                    e_store1(fin_cast)
+                if to_finish is not None:
+                    e_normalise(to_finish)
+                    e_store0(to_finish)
+                if to_cast is not None and not last:
+                    for j in range(groups[to_cast][1]):
+                        e_cast(to_cast, j, True)
+                    e_store1(to_cast)
                 if not last:
-                    run_matmuls(a - 2)
-                    fin_cast = fin_norm
-                    fin_norm = last_of.get(e + 1)
+                    pair_matmuls(a - 2)
+                    to_cast = to_finish
+                    to_finish = last_of.get(e + 1)
 
-            g_matmuls(12, 4, tp)
-            run_matmuls(12)
+            pair_matmuls(12)
+            g_matmuls(12, 4)
             for c in range(PASSES):
                 x_quantize_pass(15, c)
-            for j in range(groups[fin_cast][1]):
-                e_cast(fin_cast, j, True)
-            e_store1(fin_cast)
+            for j in range(groups[to_cast][1]):
+                e_cast(to_cast, j, True)
+            e_store1(to_cast)
             e_bias(12, 2)
             single_matmuls(14)
             single_matmuls(15)
-            e_totals(3, tp)
+            e_totals(3, 0, 2, tp, "turned2", "tot")
             e_bias(14, 1)
             e_product(12, 2)
-            e_mom0(3)
-            e_mom1(3)
+            e_moments(3)
             e_rstd(3)
             e_amax(2)
             e_bias(15, 1)
@@ -557,26 +465,24 @@ def tile_parallelretention_pb_kernel(tc, x, Wq, bq, kv, decay_mask, out_0, out_1
             e_product(15, 1)
             e_normalise(3)
             e_store0(3)
-            e_square_k(12, 2, 0)
-            e_square_k(14, 1, 0)
-            e_square_k(15, 1, 1)
-            e_total_column(4, 0)
-            e_totals(4, tp)
-            e_total_column(5, 0)
-            e_totals(5, tp)
+            e_square(12, 2)
+            e_square(14, 1)
+            e_square(15, 1)
+            e_totals(4, 0, 1, tp, "turned3", "mean")
+            e_totals(4, 0, 2, mp, "mp", "tot")
+            e_totals(5, 0, 1, mp, "mp", "mean")
+            e_totals(5, 0, 2, tp, "turned0", "tot")
             e_centre(4)
-            e_factor_v(2)
+            e_factor(2, nc.vector)
             e_amax(3)
-            e_mom0(4)
-            e_mom1(4)
+            e_moments(4)
             e_cast(2, 0, True)
             e_rstd(4)
             e_cast(2, 1, True)
             e_store1(2)
             e_centre(5)
             e_amax(4)
-            e_mom0(5)
-            e_mom1(5)
+            e_moments(5)
             e_wide(4)
             e_rstd(5)
             e_wide(5)
@@ -585,7 +491,7 @@ def tile_parallelretention_pb_kernel(tc, x, Wq, bq, kv, decay_mask, out_0, out_1
             e_scale(4)
             e_store0(4)
             e_recip(4)
-            e_factor_v(3)
+            e_factor(3, nc.vector)
             e_recip(5)
             e_scale(5)
             e_store0(5)

@@ -22,7 +22,8 @@ FLOPS = 2 * B * L * E * QD + 2 * B * L * L * QD
 GROUPS = (4, 4, 2, 2, 2, 2)
 N_RUNS = B // 2
 IN_HALVES = 4
-SORTED = (6, 8, 10, 12, 14)
+VECTOR_COPIES = ((7, 1), (11, 1))
+SORTED = (6, 10, 14)
 
 
 def tile_parallelretention_pb_kernel(tc, x, Wq, bq, kv, decay_mask, out_0, out_1):
@@ -149,7 +150,7 @@ def tile_parallelretention_pb_kernel(tc, x, Wq, bq, kv, decay_mask, out_0, out_1
         def x_copy(i, h):
             if h == 0:
                 x_tiles(i)
-            copy_out(turn_of(i), h, grouped[i])
+            copy_out(turn_of(i), h, grouped[i], (i, h) in VECTOR_COPIES)
 
         def x_quantize(i):
             nc.vector.quantize_mx(out=codes[i][:].bitcast(FP8X4), scales=scales[i][:], in_=grouped[i][:])
@@ -428,9 +429,12 @@ def tile_parallelretention_pb_kernel(tc, x, Wq, bq, kv, decay_mask, out_0, out_1
                     e_square(e, 2)
                 else:
                     e_square(e, 2)
-                    for h in range(2):
-                        x_copy(b, h)
+                    x_copy(b, 0)
+                    if (b, 1) not in VECTOR_COPIES:
+                        x_copy(b, 1)
                 x_quantize(a)
+                if (b, 1) in VECTOR_COPIES:
+                    x_copy(b, 1)
                 if to_finish is not None:
                     e_normalise(to_finish)
                     e_store0(to_finish)

@@ -428,10 +428,15 @@ def tile_parallelretention_pb_kernel(tc, x, Wq, bq, kv, decay_mask, out_0, out_1
                         x_copy_pass(b, c)
                     e_square(e, 2)
                 else:
-                    e_square(e, 2)
+                    if r not in (2, 3, 4, 5, 6):
+                        e_square(e, 2)
                     x_copy(b, 0)
+                    if r in (2, 3, 4, 5, 6):
+                        e_square(e, 2)
                     if (b, 1) not in VECTOR_COPIES:
                         x_copy(b, 1)
+                    if r not in (2, 3, 4, 5, 6):
+                        e_square(e, 2)
                 x_quantize(a)
                 if (b, 1) in VECTOR_COPIES:
                     x_copy(b, 1)

from contextlib import ExitStack

import concourse.mybir as mybir
from concourse.masks import make_block_diagonal, make_identity

F32 = mybir.dt.float32
BF16 = mybir.dt.bfloat16
U32 = mybir.dt.uint32
U8 = mybir.dt.uint8
FP8 = mybir.dt.float8_e4m3fn
FP8X4 = mybir.dt.float8_e4m3fn_x4
ALU = mybir.AluOpType
ACT = mybir.ActivationFunctionType
AXIS = mybir.AxisListType

B, L, E, QD = 16, 128, 2048, 128
EPS = 1e-5
P = 128
PASSES = E // (4 * P)
FLOPS = 2 * B * L * E * QD + 2 * B * L * L * QD

GROUPS = (4, 4, 2, 2, 2, 2)
N_RUNS = B // 2
IN_HALVES = 4
VECTOR_COPIES = ((7, 1), (11, 1))
SORTED = (6, 10, 14)


def tile_parallelretention_pb_kernel(tc, x, Wq, bq, kv, decay_mask, out_0, out_1):
    nc = tc.nc
    x_rows = x.rearrange("b h l e -> (b h l) e")
    kv_rows = kv.rearrange("b h l k -> (b h l) k")
    o0_rows = out_0.rearrange("b l q -> (b l) q")
    o1_rows = out_1.rearrange("b l q -> (b l) q")

    groups = []
    tiles = []
    for n in GROUPS:
        groups.append((P * len(tiles), n, len(tiles)))
        for j in range(n):
            tiles.append((len(groups) - 1, j))
    n_tiles = len(tiles)
    assert n_tiles == B
    last_of = dict((i0 + n - 1, g) for g, (r0, n, i0) in enumerate(groups))

    with ExitStack() as ctx:
        const = ctx.enter_context(tc.tile_pool(name="const", bufs=1))
        xin = ctx.enter_context(tc.tile_pool(name="xin", bufs=1))
        work = ctx.enter_context(tc.tile_pool(name="work", bufs=3))
        tp = ctx.enter_context(tc.psum_pool(name="tp", bufs=1))
        mp = ctx.enter_context(tc.psum_pool(name="mp", bufs=2))
        gp = ctx.enter_context(tc.psum_pool(name="gp", bufs=1))
        qp = ctx.enter_context(tc.psum_pool(name="qp", bufs=1))

        ident_b = const.tile([P, P], BF16, name="ident_b")
        ident_f = const.tile([P, P], F32, name="ident_f")
        ones_b = const.tile([P, P], BF16, name="ones_b")
        brow = const.tile([P, QD], BF16, name="brow")
        zero_col = const.tile([P, 1], F32, name="zero_col")
        one_col = const.tile([P, 1], F32, name="one_col")
        warm = const.tile([P, 1], F32, name="warm")
        nc.vector.memset(one_col[:], 1.0)
        nc.vector.memset(brow[:], 0.0)
        nc.vector.memset(ones_b[:], 1.0)
        nc.vector.memset(zero_col[:], 0.0)
        nc.scalar.activation(out=warm[:], in_=one_col[:], func=ACT.Abs_reciprocal_sqrt)
        make_identity(nc, ident_f[:])
        make_identity(nc, ident_b[:])
        mean_mask = {}
        for n in GROUPS:
            if n not in mean_mask:
                blockdiag = const.tile([P, P], F32, name="blockdiag%d" % n)
                make_block_diagonal(nc, blockdiag[:], P // n)
                mask = const.tile([P, P], F32, name="mean_mask%d" % n)
                nc.vector.tensor_scalar(out=mask[:], in0=blockdiag[:], scalar1=1.0 / (L * QD), scalar2=None, op0=ALU.mult)
                mean_mask[n] = mask

        d_in = xin.tile([P, L], BF16, name="d_in")
        kv_in = [xin.tile([P, 4, L], BF16, name="kv_in%d" % q) for q in range(n_tiles // 4)]
        w_in = [xin.tile([P, E // 2], BF16, name="w_in%d" % h) for h in range(2)]
        x_in = [
            [xin.tile([P, E // 2], BF16, name="x_in%d_%d" % (i, h)) for h in range(2)]
            if i < IN_HALVES
            else [xin.tile([P, E], BF16, name="x_in%d" % i)]
            for i in range(n_tiles)
        ]

        def x_words(i, h):
            if i < IN_HALVES:
                return x_in[i][h][:].bitcast(F32)
            return x_in[i][0][:, (E // 2) * h : (E // 2) * (h + 1)].bitcast(F32)

        kvT = [const.tile([P, 4, P], BF16, name="kvT%d" % q) for q in range(n_tiles // 4)]
        dT = const.tile([P, QD], BF16, name="dT")
        bias = const.tile([P, 2, QD], F32, name="bias")
        w_grouped = const.tile([P, E], BF16, name="w_grouped", align_bytes=64)
        w_codes = const.tile([P, E // 4], U32, name="w_codes", align_bytes=64)
        w_scales = const.tile([P, E // 4], U8, name="w_scales", align_bytes=64)

        banks = {}
        grouped = {}
        codes = {}
        scales = {}
        sorted_words = {}
        q_ps = {}
        g_ps = {}
        ep = {}

        def transposes(turn, h, words, in_order):
            tag = "turned%d" % (2 * (turn % 2) + (h + turn // 2) % 2)
            bank = tp.tile([P, 2, 2, P], F32, tag=tag, name="turned")
            for c in range(2):
                for u in range(2):
                    src = words[:, c, u, :] if in_order else words[:, 2 * P * c + u : 2 * P * (c + 1) : 2]
                    nc.tensor.transpose(bank[:, c, u, :], src, ident_f[:])
            banks[(turn, h)] = bank

        def turn_of(i):
            return i if i < 2 else i + 1

        def copy_out(turn, h, dst_tile, on_vector=False):
            dst = dst_tile[:].bitcast(F32)[:, 4 * P * h : 4 * P * (h + 1)].rearrange("p (c r u) -> p c r u", c=2, u=2)
            src = banks[(turn, h)][:].rearrange("p c u r -> p c r u")
            if on_vector:
                nc.vector.tensor_copy(out=dst, in_=src)
            else:
                nc.scalar.copy(out=dst, in_=src)

        def w_quantize():
            nc.vector.quantize_mx(out=w_codes[:].bitcast(FP8X4), scales=w_scales[:], in_=w_grouped[:])

        def x_sort(i):
            sorted_words[i] = work.tile([P, 2, 2, 2, P], F32, tag="sorted", name="sorted", bufs=2)
            for h in range(2):
                nc.vector.tensor_copy(
                    out=sorted_words[i][:, h, :, :, :], in_=x_words(i, h).rearrange("p (c r u) -> p c u r", c=2, u=2)
                )

        def x_transposes(i, h):
            if i in SORTED:
                transposes(turn_of(i), h, sorted_words[i][:, h, :, :, :], True)
            else:
                transposes(turn_of(i), h, x_words(i, h), False)

        def x_tiles(i):
            grouped[i] = work.tile([P, E], BF16, tag="grouped", name="grouped", bufs=4, align_bytes=64)
            codes[i] = const.tile([P, E // 4], U32, name="codes%d" % i, align_bytes=64)
            scales[i] = const.tile([P, E // 4], U8, name="scales%d" % i, align_bytes=64)

        def x_copy(i, h):
            if h == 0:
                x_tiles(i)
            copy_out(turn_of(i), h, grouped[i], (i, h) in VECTOR_COPIES)

        def x_quantize(i):
            nc.vector.quantize_mx(out=codes[i][:].bitcast(FP8X4), scales=scales[i][:], in_=grouped[i][:])

        def x_copy_pass(i, c):
            if c == 0:
                x_tiles(i)
            dst = grouped[i][:].bitcast(F32)[:, 2 * P * c : 2 * P * (c + 1)].rearrange("p (r u) -> p r u", u=2)
            nc.scalar.copy(out=dst, in_=banks[(turn_of(i), c // 2)][:, c % 2, :, :].rearrange("p u r -> p r u"))

        def x_quantize_pass(i, c):
            cols = slice(c * P, (c + 1) * P)
            nc.vector.quantize_mx(
                out=codes[i][:, cols].bitcast(FP8X4), scales=scales[i][:, cols], in_=grouped[i][:, 4 * P * c : 4 * P * (c + 1)]
            )

        def kv_transposes(q):
            banks[("kv", q)] = mp.tile([P, 4, P], BF16, tag="mp", name="kvT_ps")
            for j in range(4):
                nc.tensor.transpose(banks[("kv", q)][:, j, :], kv_in[q][:, j, :], ident_b[:])

        def kv_copy(q):
            nc.vector.tensor_copy(out=kvT[q][:], in_=banks[("kv", q)][:])

        def d_transpose():
            banks["d"] = mp.tile([P, QD], BF16, tag="mp", name="dT_ps")
            nc.tensor.transpose(banks["d"][:], d_in[:], ident_b[:])

        def d_copy():
            nc.vector.tensor_copy(out=dT[:], in_=banks["d"][:])

        def bias_matmul():
            banks["b"] = gp.tile([P, QD], F32, tag="g", name="b_ps")
            nc.tensor.matmul(out=banks["b"][:], lhsT=ones_b[:], rhs=brow[:], start=True, stop=True)

        def bias_copies():
            for j in range(2):
                nc.vector.tensor_copy(out=bias[:, j, :], in_=banks["b"][:])

        def g_matmuls(i, n):
            bank = gp.tile([P, n, QD], F32, tag="g", name="g_ps")
            for k in range(n):
                nc.tensor.matmul(
                    out=bank[:, k, :], lhsT=kvT[(i + k) // 4][:, (i + k) % 4, :], rhs=dT[:], start=True, stop=True
                )
                g_ps[i + k] = (bank, k)

        def x_matmuls(i, out):
            for c in range(PASSES):
                cols = slice(c * P, (c + 1) * P)
                nc.tensor.matmul_mx(
                    out=out,
                    lhsT=codes[i][:, cols].bitcast(FP8X4),
                    lhsT_scale=scales[i][:, cols],
                    rhs=w_codes[:, cols].bitcast(FP8X4),
                    rhs_scale=w_scales[:, cols],
                    start=(c == 0),
                    stop=(c == PASSES - 1),
                )

        def pair_matmuls(i):
            q = qp.tile([P, 2, QD], F32, tag="q", name="q_ps")
            for k in (1, 0):
                x_matmuls(i + k, q[:, k, :])
            q_ps[(i, 2)] = q[:]

        def single_matmuls(i):
            q = mp.tile([P, 1, QD], F32, tag="mp", name="q_single")
            x_matmuls(i, q[:, 0, :])
            q_ps[(i, 1)] = q[:]

        def e_bias(i, n):
            g, j = tiles[i]
            if j == 0:
                ep[("t", g)] = work.tile([P, groups[g][1], QD], F32, tag="t", name="t", bufs=6)
                ep[("y", g)] = work.tile([P, groups[g][1], QD], F32, tag="y", name="y", bufs=6)
                ep[("sums", g)] = []
            nc.vector.tensor_tensor(out=ep[("t", g)][:, j : j + n, :], in0=q_ps[(i, n)], in1=bias[:, 0:n, :], op=ALU.add)

        def e_product(i, n):
            g, j = tiles[i]
            bank, k = g_ps[i]
            sums = work.tile([P, 2], F32, tag="sums", name="sums", bufs=6)
            nc.vector.scalar_tensor_tensor(
                out=ep[("y", g)][:, j : j + n, :], in0=ep[("t", g)][:, j : j + n, :], scalar=1.0,
                in1=bank[:, k : k + n, :], op0=ALU.mult, op1=ALU.mult, accum_out=sums[:, 0:1],
            )
            ep[("part", i)] = sums
            ep[("sums", g)].append(sums)

        def e_square(i, n):
            g, j = tiles[i]
            junk = work.tile([P, n, QD], F32, tag="junk", name="junk")
            nc.scalar.activation(
                out=junk[:], in_=ep[("y", g)][:, j : j + n, :], func=ACT.Square, accum_out=ep[("part", i)][:, 1:2]
            )

        def e_totals(g, first, n_cols, pool, tag, key):
            tot = pool.tile([P, n_cols], F32, tag=tag, name="tot")
            parts = ep[("sums", g)]
            for k, sums in enumerate(parts):
                nc.tensor.matmul(
                    out=tot[:], lhsT=mean_mask[groups[g][1]][:], rhs=sums[:, first : first + n_cols], start=(k == 0),
                    stop=(k == len(parts) - 1),
                )
            ep[(key, g)] = tot

        def e_moments(g):
            ep[("neg_mean", g)] = work.tile([P, 1], F32, tag="neg_mean", name="neg_mean")
            ep[("square", g)] = work.tile([P, 1], F32, tag="square", name="square")
            nc.scalar.activation(out=ep[("neg_mean", g)][:], in_=ep[("tot", g)][:, 0:1], func=ACT.Copy, scale=-1.0)
            nc.scalar.activation(out=ep[("square", g)][:], in_=ep[("tot", g)][:, 1:2], func=ACT.Copy, bias=EPS)

        def e_rstd(g):
            ep[("rstd", g)] = work.tile([P, 1], F32, tag="rstd", name="rstd")
            nc.scalar.activation(
                out=ep[("rstd", g)][:], in_=ep[("tot", g)][:, 0:1], func=ACT.Abs_reciprocal_sqrt, bias=ep[("square", g)][:],
                scale=ep[("neg_mean", g)][:],
            )

        def e_normalise(g):
            ep[("res", g)] = work.tile([P, groups[g][1], QD], F32, tag="res", name="res", bufs=6)
            nc.vector.tensor_scalar(
                out=ep[("res", g)][:], in0=ep[("y", g)][:], scalar1=ep[("neg_mean", g)][:], scalar2=ep[("rstd", g)][:],
                op0=ALU.add, op1=ALU.mult,
            )

        def e_centre(g):
            ep[("d", g)] = work.tile([P, groups[g][1], QD], F32, tag="d", name="d")
            nc.vector.tensor_scalar(
                out=ep[("d", g)][:], in0=ep[("y", g)][:], scalar1=ep[("mean", g)][:], scalar2=None, op0=ALU.subtract
            )

        def e_scale(g):
            ep[("res", g)] = work.tile([P, groups[g][1], QD], F32, tag="res", name="res", bufs=6)
            nc.vector.tensor_scalar(
                out=ep[("res", g)][:], in0=ep[("d", g)][:], scalar1=ep[("rstd", g)][:], scalar2=None, op0=ALU.mult
            )

        def e_wide(g):
            ep[("wide", g)] = work.tile([P, groups[g][1], QD], F32, tag="wide", name="wide")
            nc.scalar.activation(out=ep[("wide", g)][:], in_=ep[("d", g)][:], func=ACT.Copy, scale=448.0)

        def e_store0(g):
            r0, n, i0 = groups[g]
            nc.sync.dma_start(out=o0_rows[r0 : r0 + P * n, :].rearrange("(p j) q -> p j q", j=n), in_=ep[("res", g)][:])

        def e_amax(g):
            ep[("amax", g)] = work.tile([P, groups[g][1]], F32, tag="amax", name="amax")
            src = ep[("d", g)] if ("d", g) in ep else ep[("res", g)]
            nc.vector.tensor_reduce(out=ep[("amax", g)][:], in_=src[:], axis=AXIS.X, op=ALU.max, apply_absolute_value=True)

        def e_recip(g):
            ep[("ramax", g)] = work.tile([P, groups[g][1]], F32, tag="ramax", name="ramax")
            nc.vector.reciprocal(out=ep[("ramax", g)][:], in_=ep[("amax", g)][:])

        def e_factor(g, eng):
            ep[("factor", g)] = work.tile([P, groups[g][1]], F32, tag="factor", name="factor")
            eng.tensor_scalar(
                out=ep[("factor", g)][:], in0=ep[("ramax", g)][:], scalar1=448.0, scalar2=0.0, op0=ALU.mult, op1=ALU.add
            )

        def e_cast(g, j, on_scalar):
            if ("o8", g) not in ep:
                ep[("o8", g)] = work.tile([P, groups[g][1], QD], FP8, tag="o8", name="o8", bufs=6)
            dst = ep[("o8", g)][:, j, :]
            src = ep[("wide", g)] if ("wide", g) in ep else ep[("res", g)]
            factor = ep[("ramax", g)] if ("wide", g) in ep else ep[("factor", g)]
            if on_scalar:
                nc.scalar.activation(
                    out=dst, in_=src[:, j, :], func=ACT.Identity, bias=zero_col[:], scale=factor[:, j : j + 1], saturate=False
                )
            else:
                nc.vector.tensor_scalar(
                    out=dst, in0=src[:, j, :], scalar1=factor[:, j : j + 1], scalar2=None, op0=ALU.mult, saturate=False
                )

        def e_store1(g):
            r0, n, i0 = groups[g]
            nc.sync.dma_start(
                out=o1_rows[r0 : r0 + P * n, :].rearrange("(p j) q -> p (j q)", j=n),
                in_=ep[("o8", g)][:].bitcast(U8).rearrange("p j q -> p (j q)"),
            )

        def load_x(i):
            g, j = tiles[i]
            r0, n, i0 = groups[g]
            rows = x_rows[r0 : r0 + P * n, :].rearrange("(p j) e -> p j e", j=n)
            if i < IN_HALVES:
                for h in range(2):
                    nc.sync.dma_start(out=x_in[i][h][:], in_=rows[:, j, (E // 2) * h : (E // 2) * (h + 1)])
            else:
                nc.sync.dma_start(out=x_in[i][0][:], in_=rows[:, j, :])

        def load_kv(q):
            n = groups[tiles[4 * q][0]][1]
            nc.sync.dma_start(
                out=kv_in[q][:].rearrange("p (s j) k -> p s (j k)", j=n),
                in_=kv_rows[4 * P * q : 4 * P * (q + 1), :].rearrange("(s p j) k -> p s (j k)", p=P, j=n),
            )

        with tc.manual_schedule():
            load_x(0)
            load_x(1)
            for h in range(2):
                nc.sync.dma_start(out=w_in[h][:], in_=Wq[:, (E // 2) * h : (E // 2) * (h + 1)])
            load_kv(0)
            nc.sync.dma_start(out=d_in[:], in_=decay_mask.rearrange("o j i -> (o j) i"))
            nc.sync.dma_start(out=brow[0:1, :], in_=bq.rearrange("(o q) -> o q", o=1))
            for i in range(2, n_tiles):
                if i > 2 and i % 4 == 0:
                    load_kv(i // 4)
                load_x(i)

            for i in range(2):
                for h in range(2):
                    x_transposes(i, h)
                    x_copy(i, h)
                if i == 0:
                    x_quantize(i)
            for h in range(2):
                transposes(2, h, w_in[h][:].bitcast(F32), False)
                copy_out(2, h, w_grouped, h == 0)
            x_quantize(1)
            kv_transposes(0)
            kv_copy(0)
            d_transpose()
            d_copy()
            bias_matmul()
            bias_copies()
            w_quantize()
            for i in (2, 3):
                for h in range(2):
                    x_transposes(i, h)
                    x_copy(i, h)
                if i == 2:
                    x_quantize(i)
            pair_matmuls(0)

            to_finish = None
            to_cast = None
            for r in range(2, N_RUNS):
                a, b, e = 2 * r, 2 * r + 1, 2 * (r - 2)
                last = r == N_RUNS - 1
                if a % 4 == 0:
                    kv_transposes(a // 4)
                x_transposes(a, 0)
                if to_finish is not None:
                    e_totals(to_finish, 0, 2, mp, "mp", "tot")
                x_transposes(a, 1)
                g_matmuls(e, 2)
                x_copy(a, 0)
                if to_finish is not None:
                    e_moments(to_finish)
                x_copy(a, 1)
                if to_finish is not None:
                    e_rstd(to_finish)
                e_bias(e, 2)
                if a % 4 == 0:
                    kv_copy(a // 4)
                x_quantize(b - 2)
                if to_cast is not None:
                    e_amax(to_cast)
                e_product(e, 2)
                for i in (a + 2, b + 2):
                    if i in SORTED:
                        x_sort(i)
                if to_cast is not None:
                    e_recip(to_cast)
                    e_factor(to_cast, nc.gpsimd)
                x_transposes(b, 0)
                x_transposes(b, 1)
                if last:
                    for c in range(PASSES):
                        x_copy_pass(b, c)
                    e_square(e, 2)
                else:
                    if r not in (2, 3, 4, 5, 6):
                        e_square(e, 2)
                    x_copy(b, 0)
                    if r in (2, 3, 4, 5, 6):
                        e_square(e, 2)
                    if (b, 1) not in VECTOR_COPIES:
                        x_copy(b, 1)
                    if r not in (2, 3, 4, 5, 6):
                        e_square(e, 2)
                x_quantize(a)
                if (b, 1) in VECTOR_COPIES:
                    x_copy(b, 1)
                if to_finish is not None:
                    e_normalise(to_finish)
                    e_store0(to_finish)
                if to_cast is not None and not last:
                    for j in range(groups[to_cast][1]):
                        e_cast(to_cast, j, True)
                    e_store1(to_cast)
                if not last:
                    pair_matmuls(a - 2)
                    to_cast = to_finish
                    to_finish = last_of.get(e + 1)

            pair_matmuls(12)
            g_matmuls(12, 4)
            for c in range(PASSES):
                x_quantize_pass(15, c)
            for j in range(groups[to_cast][1]):
                e_cast(to_cast, j, True)
            e_store1(to_cast)
            e_bias(12, 2)
            single_matmuls(14)
            single_matmuls(15)
            e_totals(3, 0, 2, tp, "turned2", "tot")
            e_bias(14, 1)
            e_product(12, 2)
            e_moments(3)
            e_rstd(3)
            e_amax(2)
            e_bias(15, 1)
            e_product(14, 1)
            e_recip(2)
            e_product(15, 1)
            e_normalise(3)
            e_store0(3)
            e_square(12, 2)
            e_square(14, 1)
            e_square(15, 1)
            e_totals(4, 0, 1, tp, "turned3", "mean")
            e_totals(4, 0, 2, mp, "mp", "tot")
            e_totals(5, 0, 1, mp, "mp", "mean")
            e_totals(5, 0, 2, tp, "turned0", "tot")
            e_centre(4)
            e_factor(2, nc.vector)
            e_amax(3)
            e_moments(4)
            e_cast(2, 0, True)
            e_rstd(4)
            e_cast(2, 1, True)
            e_store1(2)
            e_centre(5)
            e_amax(4)
            e_moments(5)
            e_wide(4)
            e_rstd(5)
            e_wide(5)
            e_recip(3)
            e_amax(5)
            e_scale(4)
            e_store0(4)
            e_recip(4)
            e_factor(3, nc.vector)
            e_recip(5)
            e_scale(5)
            e_store0(5)
            e_cast(4, 0, True)
            e_cast(3, 0, False)
            e_cast(3, 1, False)
            e_store1(3)
            e_cast(4, 1, True)
            e_store1(4)
            e_cast(5, 0, True)
            e_cast(5, 1, False)
            e_store1(5)
